import numpy as np
import ml_dtypes


def mxq(x, axis, fmt="e4m3"):
    dtype, down = {"e4m3": (ml_dtypes.float8_e4m3fn, 7), "e5m2": (ml_dtypes.float8_e5m2, 14)}[fmt]
    v = np.moveaxis(np.asarray(x, np.float32).astype(ml_dtypes.bfloat16).astype(np.float64), axis, -1)
    blocks = v.reshape(v.shape[:-1] + (-1, 32))
    amax = np.abs(blocks).max(-1, keepdims=True)
    byte = np.maximum(np.where(amax > 0, np.frexp(amax)[1] - 1 + 127, 0) - down, 1)
    scale = np.exp2(byte - 127.0)
    codes = (blocks / scale).astype(np.float32).astype(dtype).astype(np.float64)
    return np.moveaxis((codes * scale).reshape(v.shape), -1, axis)


WIDE = False


def mx_kscale(k):
    if not WIDE:
        return np.ones(k)
    levels = np.array([10, -10, 5, -5, 0])
    a = np.random.permutation(np.resize(levels, k // 512 * 4)).reshape(k // 512, 4)
    idx = np.arange(k)
    return np.exp2(a[idx // 512, idx % 128 // 32])


BF16 = ml_dtypes.bfloat16


def bf(x):
    return np.asarray(x, np.float32).astype(BF16)


def f64(x):
    return np.asarray(x).astype(np.float64)


B, L, S, D, H = 4, 1536, 512, 512, 1
ITER = 3
E = D // H
QS = 1.4 / E ** 0.25


def setup_inputs():
    s = np.tile(mx_kscale(E), H)
    t = mx_kscale(D)
    q = (np.random.standard_normal((B, L, D)) + 0.35 * np.random.standard_normal(D)) * QS
    k = (np.random.standard_normal((B, S, D)) + 0.35 * np.random.standard_normal(D)) * QS
    return {"q_proj": bf(q * s), "k_proj": bf(k / s),
            "values": bf(np.random.standard_normal((B, S, D)) * t),
            "Wv": bf(np.random.standard_normal((D, D)) / np.sqrt(D) / t[:, None]),
            "bv": bf(np.random.standard_normal(D) * 0.2)}


def reference(q_proj, k_proj, values, Wv, bv):
    qh = mxq(f64(q_proj).reshape(B, L, H, E).transpose(0, 2, 1, 3), 3, "e4m3")
    kh = mxq(f64(k_proj).reshape(B, S, H, E).transpose(0, 2, 3, 1), 2, "e4m3")
    v = ((mxq(f64(values), 2, "e4m3") @ mxq(f64(Wv), 0, "e4m3")) + f64(bv)).reshape(B, S, H, E)
    attn_list = []
    acc = np.zeros((B, S, H, E))
    for i in range(ITER):
        stride = i + 1
        attn = qh[:, :, ::stride] @ kh
        attn_list.append(attn)
        e = np.exp(attn - attn.max(-1, keepdims=True))
        att = e / e.sum(-1, keepdims=True)
        colsum = att.sum(2)
        acc = acc + v * colsum.transpose(0, 2, 1)[..., None]
    return ((acc / ITER).reshape(B, S, D), *attn_list)

@@ -1,0 +1,344 @@
+from contextlib import ExitStack
+
+import concourse.mybir as mybir
+from concourse.masks import make_identity
+
+F32 = mybir.dt.float32
+BF16 = mybir.dt.bfloat16
+U32 = mybir.dt.uint32
+U8 = mybir.dt.uint8
+FP8X4 = mybir.dt.float8_e4m3fn_x4
+ALU = mybir.AluOpType
+FUNC = mybir.ActivationFunctionType
+
+P = 128
+BATCH = 4
+QUERIES = 1536
+KEYS = 512
+WIDTH = 512
+STRIDES = (1, 2, 3)
+
+PACK = 4
+HALVES = 2
+ROWS = 4
+QUERY_TILES = QUERIES // P
+KEY_TILES = KEYS // P
+GROUPS_PER_BATCH = QUERY_TILES // ROWS
+N_GROUPS = BATCH * GROUPS_PER_BATCH
+VECTOR_TILES = 2
+
+FLOPS = 2 * BATCH * (QUERIES * KEYS * WIDTH + KEYS * WIDTH * WIDTH)
+
+
+def tile_trendattentionlayer_pa_t_kernel(
+    tc, q_proj, k_proj, values, Wv, bv, out, attn_1, attn_2, attn_3
+):
+    nc = tc.nc
+    attn_out = {1: attn_1, 2: attn_2, 3: attn_3}
+
+    with ExitStack() as stack:
+        const = stack.enter_context(tc.tile_pool(name="const", bufs=1))
+        loaded = stack.enter_context(tc.tile_pool(name="loaded", bufs=1))
+        operands = stack.enter_context(tc.tile_pool(name="operands", bufs=2))
+        results = stack.enter_context(tc.tile_pool(name="results", bufs=2))
+        stats = stack.enter_context(tc.tile_pool(name="stats", bufs=3))
+        transposed = stack.enter_context(tc.psum_pool(name="transposed", bufs=2))
+        products = stack.enter_context(tc.psum_pool(name="products", bufs=5))
+        gate_banks = stack.enter_context(tc.psum_pool(name="gate_banks", bufs=1))
+        stack.enter_context(tc.manual_schedule())
+
+        def load_rows(rows, name, copies):
+            raw = loaded.tile([P, ROWS * WIDTH], BF16, name=name, bufs=copies)
+            nc.sync.dma_start(out=raw[:].rearrange("p (r e) -> p r e", r=ROWS), in_=rows)
+            return raw
+
+        query_raw, key_raw, value_raw = {}, {}, {}
+        weight_raw = loaded.tile([P, PACK * WIDTH], BF16, name="weight_raw")
+        bias = const.tile([P, WIDTH], BF16, name="bias")
+        for b in range(BATCH):
+            queries = q_proj[b].rearrange("(p j) e -> p j e", j=QUERY_TILES)
+            for h in range(GROUPS_PER_BATCH):
+                if h == 0:
+                    key_raw[b] = load_rows(
+                        k_proj[b].rearrange("(p r) e -> p r e", r=ROWS), "key_raw", BATCH
+                    )
+                query_raw[b * GROUPS_PER_BATCH + h] = load_rows(
+                    queries[:, h * ROWS : (h + 1) * ROWS, :], "query_raw", N_GROUPS
+                )
+            value_raw[b] = load_rows(
+                values[b].rearrange("(p r) e -> p r e", r=ROWS), "value_raw", BATCH
+            )
+            if b == 0:
+                nc.sync.dma_start(
+                    out=weight_raw[:].rearrange("w (u e n) -> w u e n", u=HALVES, e=2),
+                    in_=Wv.rearrange("(u w e) n -> w u e n", u=HALVES, e=2),
+                )
+                nc.sync.dma_start(out=bias[:], in_=bv.partition_broadcast(P))
+
+        identity = const.tile([P, P], F32, name="identity")
+        make_identity(nc, identity[:])
+        ones_f32 = const.tile([P, P], F32, name="ones_f32")
+        nc.gpsimd.memset(ones_f32[:], 1.0)
+        uses = const.tile([P, QUERY_TILES], F32, name="uses")
+        nc.vector.memset(uses[:], 1.0)
+        nc.vector.memset(uses[:, 0:QUERY_TILES:2], 2.0)
+        nc.vector.memset(uses[:, 3:QUERY_TILES:6], 2.0)
+        nc.vector.memset(uses[:, 0:QUERY_TILES:6], 3.0)
+        warm = const.tile([P, 1], F32, name="warm")
+        nc.vector.memset(warm[:], 0.0)
+        warmed = const.tile([P, 1], F32, name="warmed")
+        nc.scalar.activation(out=warmed[:], in_=warm[:], func=FUNC.Exp)
+
+        def transpose_rows(raw, name, columns_by_row):
+            grouped = operands.tile([P, ROWS * P * PACK], BF16, name=name, align_bytes=64)
+            raw_words = raw[:].bitcast(F32)
+            grouped_words = grouped[:].bitcast(F32)
+            for first in range(0, ROWS, 2):
+                bank = transposed.tile([P, 2 * HALVES * P], F32, name="bank")
+                for slot in range(2 * HALVES):
+                    source = (first * HALVES + slot) * P
+                    nc.tensor.transpose(
+                        bank[:, slot * P : (slot + 1) * P],
+                        raw_words[:, source : source + P],
+                        identity[:],
+                    )
+                if columns_by_row:
+                    nc.scalar.copy(
+                        out=grouped_words.rearrange("w (r p u) -> w r p u", r=ROWS, u=HALVES)[
+                            :, first : first + 2, :, :
+                        ],
+                        in_=bank[:].rearrange("w (r u p) -> w r p u", r=2, u=HALVES),
+                    )
+                else:
+                    nc.scalar.copy(
+                        out=grouped_words.rearrange("w (p r u) -> w p r u", r=ROWS, u=HALVES)[
+                            :, :, first : first + 2, :
+                        ],
+                        in_=bank[:].rearrange("w (r u p) -> w p r u", r=2, u=HALVES),
+                    )
+            return grouped
+
+        def quantise(grouped, name, copies):
+            codes = operands.tile([P, ROWS * P], U32, name=name + "_codes", bufs=copies, align_bytes=64)
+            scales = operands.tile([P, ROWS * P], U8, name=name + "_scales", bufs=copies, align_bytes=64)
+            nc.vector.quantize_mx(out=codes[:].bitcast(FP8X4), scales=scales[:], in_=grouped[:])
+            return codes, scales
+
+        query_grouped, key_grouped, value_grouped = {}, {}, {}
+        query_mx, key_mx, value_mx, weight_mx = {}, {}, {}, {}
+
+        def transpose_queries(g):
+            if 0 <= g < N_GROUPS:
+                query_grouped[g] = transpose_rows(query_raw[g], "query_grouped", True)
+
+        def quantise_queries(g):
+            if 0 <= g < N_GROUPS:
+                query_mx[g] = quantise(query_grouped[g], "query", 3)
+
+        def transpose_keys(b):
+            if 0 <= b < BATCH:
+                key_grouped[b] = transpose_rows(key_raw[b], "key_value_grouped", False)
+
+        def quantise_keys(b):
+            if 0 <= b < BATCH:
+                key_mx[b] = quantise(key_grouped[b], "key", 2)
+
+        def transpose_values(b):
+            if 0 <= b < BATCH:
+                value_grouped[b] = transpose_rows(value_raw[b], "key_value_grouped", False)
+
+        def quantise_values(b):
+            if 0 <= b < BATCH:
+                value_mx[b] = quantise(value_grouped[b], "value", 2)
+
+        scores, tops, shifts, exponentials, shares = {}, {}, {}, {}, {}
+        partial_sums, gate_rows, gate_copies, projected = {}, {}, {}, {}
+
+        def multiply_scores(g, r):
+            if not 0 <= g < N_GROUPS:
+                return
+            if r == 0:
+                scores[g] = results.tile([P, ROWS, KEYS], F32, name="attn", bufs=6)
+                tops[g] = stats.tile([P, ROWS], F32, name="top")
+            codes, scales = query_mx[g]
+            key_codes, key_scales = key_mx[g // GROUPS_PER_BATCH]
+            cols = slice(r * P, (r + 1) * P)
+            acc = products.tile([P, KEYS], F32, name="acc")
+            nc.tensor.matmul_mx(
+                out=acc[:],
+                lhsT=codes[:, cols].bitcast(FP8X4),
+                lhsT_scale=scales[:, cols],
+                rhs=key_codes[:].bitcast(FP8X4),
+                rhs_scale=key_scales[:],
+                start=True,
+                stop=True,
+            )
+            nc.vector.tensor_scalar(
+                out=scores[g][:, r, :],
+                in0=acc[:],
+                scalar1=1.0,
+                scalar2=None,
+                op0=ALU.mult,
+                op1=ALU.max,
+                accum_out=tops[g][:, r : r + 1],
+            )
+
+        def store_scores(g):
+            if not 0 <= g < N_GROUPS:
+                return
+            b, h = divmod(g, GROUPS_PER_BATCH)
+            shifts[g] = stats.tile([P, ROWS], F32, name="shift")
+            nc.vector.tensor_scalar_mul(out=shifts[g][:], in0=tops[g][:], scalar1=-1.0)
+            for stride in STRIDES:
+                first = (-h * ROWS) % stride
+                count = len(range(first, ROWS, stride))
+                start_row = (h * ROWS + first) // stride
+                rows = attn_out[stride][b, 0].rearrange("(p r) s -> p r s", r=QUERY_TILES // stride)
+                nc.sync.dma_start(
+                    out=rows[:, start_row : start_row + count, :],
+                    in_=scores[g][:, first:ROWS:stride, :],
+                )
+
+        def exponentiate(g):
+            if not 0 <= g < N_GROUPS:
+                return
+            h = g % GROUPS_PER_BATCH
+            e = results.tile([P, ROWS, KEYS], F32, name="e", bufs=3)
+            z = stats.tile([P, ROWS], F32, name="z")
+            for r in range(ROWS):
+                nc.scalar.activation(
+                    out=e[:, r, :],
+                    in_=scores[g][:, r, :],
+                    func=FUNC.Exp,
+                    bias=shifts[g][:, r : r + 1],
+                    scale=1.0,
+                    accum_out=z[:, r : r + 1],
+                )
+            inverse = stats.tile([P, ROWS], F32, name="inverse")
+            nc.vector.reciprocal(out=inverse[:], in_=z[:])
+            share = stats.tile([P, ROWS], F32, name="share")
+            nc.vector.tensor_mul(out=share[:], in0=inverse[:], in1=uses[:, h * ROWS : (h + 1) * ROWS])
+            exponentials[g], shares[g] = e, share
+
+        def add_on_vector(g, r):
+            if not 0 <= g < N_GROUPS:
+                return
+            b, h = divmod(g, GROUPS_PER_BATCH)
+            if h == 0 and r == 0:
+                partial_sums[b] = results.tile([P, KEYS], F32, name="partial_sum")
+                nc.vector.tensor_scalar_mul(
+                    out=partial_sums[b][:],
+                    in0=exponentials[g][:, r, :],
+                    scalar1=shares[g][:, r : r + 1],
+                )
+            else:
+                nc.vector.scalar_tensor_tensor(
+                    out=partial_sums[b][:],
+                    in0=exponentials[g][:, r, :],
+                    scalar=shares[g][:, r : r + 1],
+                    in1=partial_sums[b][:],
+                    op0=ALU.mult,
+                    op1=ALU.add,
+                )
+
+        def add_on_tensor(g):
+            if not 0 <= g < N_GROUPS:
+                return
+            b, h = divmod(g, GROUPS_PER_BATCH)
+            if h == 0:
+                gate_rows[b] = gate_banks.tile([P, KEYS], F32, name="gate_row")
+            for r in range(VECTOR_TILES, ROWS):
+                nc.tensor.matmul(
+                    out=gate_rows[b][:],
+                    lhsT=shares[g][:, r : r + 1].to_broadcast([P, P]),
+                    rhs=exponentials[g][:, r, :],
+                    start=(h == 0 and r == VECTOR_TILES),
+                    stop=False,
+                )
+
+        def close_sums(b):
+            if not 0 <= b < BATCH:
+                return
+            nc.tensor.matmul(
+                out=gate_rows[b][:], lhsT=ones_f32[:], rhs=partial_sums[b][:], start=False, stop=True
+            )
+            gate_copies[b] = results.tile([P, KEYS], F32, name="gate_copy")
+            nc.scalar.copy(out=gate_copies[b][:], in_=gate_rows[b][:])
+
+        def quantise_weights():
+            weight_grouped = operands.tile([P, WIDTH * PACK], BF16, name="weight_grouped", bufs=1, align_bytes=64)
+            nc.vector.tensor_copy(
+                out=weight_grouped[:].rearrange("w (n t) -> w n t", t=PACK),
+                in_=weight_raw[:].rearrange("w (t n) -> w n t", t=PACK),
+            )
+            weight_mx[0] = quantise(weight_grouped, "weight", 1)
+
+        def project_values(b):
+            if not 0 <= b < BATCH:
+                return
+            codes, scales = value_mx[b]
+            weight_codes, weight_scales = weight_mx[0]
+            v = results.tile([P, KEY_TILES, WIDTH], F32, name="v", bufs=2)
+            for i in range(KEY_TILES):
+                cols = slice(i * P, (i + 1) * P)
+                acc = products.tile([P, WIDTH], F32, name="acc")
+                nc.tensor.matmul_mx(
+                    out=acc[:],
+                    lhsT=codes[:, cols].bitcast(FP8X4),
+                    lhsT_scale=scales[:, cols],
+                    rhs=weight_codes[:].bitcast(FP8X4),
+                    rhs_scale=weight_scales[:],
+                    start=True,
+                    stop=True,
+                )
+                nc.vector.tensor_tensor(out=v[:, i, :], in0=acc[:], in1=bias[:], op=ALU.add)
+            projected[b] = v
+
+        def finish(b):
+            if not 0 <= b < BATCH:
+                return
+            bank = transposed.tile([P, KEY_TILES * P], F32, name="bank")
+            for i in range(KEY_TILES):
+                cols = slice(i * P, (i + 1) * P)
+                nc.tensor.transpose(bank[:, cols], gate_copies[b][:, cols], identity[:])
+            gate = stats.tile([P, KEY_TILES], F32, name="gate")
+            nc.vector.tensor_scalar_mul(
+                out=gate[:], in0=bank[:, 0 : KEY_TILES * P : P], scalar1=1.0 / len(STRIDES)
+            )
+            v = projected[b]
+            for i in range(KEY_TILES):
+                if i % 2 == 0:
+                    nc.scalar.activation(
+                        out=v[:, i, :], in_=v[:, i, :], func=FUNC.Copy, scale=gate[:, i : i + 1]
+                    )
+                else:
+                    nc.vector.tensor_scalar_mul(
+                        out=v[:, i, :], in0=v[:, i, :], scalar1=gate[:, i : i + 1]
+                    )
+            nc.sync.dma_start(out=out[b].rearrange("(i p) e -> p i e", p=P), in_=v[:])
+
+        for t in range(-3, N_GROUPS + 3):
+            b, h = divmod(t, GROUPS_PER_BATCH)
+            if h == 1:
+                quantise_keys(b + 1)
+            quantise_queries(t + 1)
+            for r in range(ROWS):
+                multiply_scores(t, r)
+                if r < VECTOR_TILES:
+                    add_on_vector(t - 2, r)
+            store_scores(t)
+            exponentiate(t - 1)
+            transpose_queries(t + 2)
+            if h == 1:
+                project_values(b)
+            add_on_tensor(t - 2)
+            if h == 0:
+                if b == 0:
+                    quantise_weights()
+                quantise_values(b)
+                transpose_keys(b + 1)
+            if h == 1:
+                close_sums(b - 1)
+            if h == 2:
+                transpose_values(b + 1)
+                finish(b - 1)

@@ -294,31 +294,33 @@ def tile_trendattentionlayer_pa_t_kernel(
                 nc.vector.tensor_tensor(out=v[:, i, :], in0=acc[:], in1=bias[:], op=ALU.add)
             projected[b] = v
 
-        def finish(b):
+        gates = {}
+
+        def transpose_gate(b):
             if not 0 <= b < BATCH:
                 return
             bank = transposed.tile([P, KEY_TILES * P], F32, name="bank")
             for i in range(KEY_TILES):
                 cols = slice(i * P, (i + 1) * P)
                 nc.tensor.transpose(bank[:, cols], gate_copies[b][:, cols], identity[:])
-            gate = stats.tile([P, KEY_TILES], F32, name="gate")
+            gates[b] = stats.tile([P, KEY_TILES], F32, name="gate")
             nc.vector.tensor_scalar_mul(
-                out=gate[:], in0=bank[:, 0 : KEY_TILES * P : P], scalar1=1.0 / len(STRIDES)
+                out=gates[b][:], in0=bank[:, 0 : KEY_TILES * P : P], scalar1=1.0 / len(STRIDES)
             )
+
+        def apply_gate(b):
+            if not 0 <= b < BATCH:
+                return
             v = projected[b]
             for i in range(KEY_TILES):
-                if i % 2 == 0:
-                    nc.scalar.activation(
-                        out=v[:, i, :], in_=v[:, i, :], func=FUNC.Copy, scale=gate[:, i : i + 1]
-                    )
-                else:
-                    nc.vector.tensor_scalar_mul(
-                        out=v[:, i, :], in0=v[:, i, :], scalar1=gate[:, i : i + 1]
-                    )
+                nc.scalar.activation(
+                    out=v[:, i, :], in_=v[:, i, :], func=FUNC.Copy, scale=gates[b][:, i : i + 1]
+                )
             nc.sync.dma_start(out=out[b].rearrange("(i p) e -> p i e", p=P), in_=v[:])
 
-        for t in range(-3, N_GROUPS + 3):
+        for t in range(-3, N_GROUPS + 4):
             b, h = divmod(t, GROUPS_PER_BATCH)
+            value_batch, value_step = divmod(t + 1, 4)
             if h == 1:
                 quantise_keys(b + 1)
             quantise_queries(t + 1)
@@ -328,17 +330,21 @@ def tile_trendattentionlayer_pa_t_kernel(
                     add_on_vector(t - 2, r)
             store_scores(t)
             exponentiate(t - 1)
-            transpose_queries(t + 2)
-            if h == 1:
-                project_values(b)
-            add_on_tensor(t - 2)
             if h == 0:
-                if b == 0:
+                apply_gate(b - 2)
+            transpose_queries(t + 2)
+            add_on_tensor(t - 2)
+            if value_step == 2:
+                project_values(value_batch)
+            if value_step == 1:
+                if value_batch == 0:
                     quantise_weights()
-                quantise_values(b)
+                quantise_values(value_batch)
+            if h == 0:
                 transpose_keys(b + 1)
+            if value_step == 0:
+                transpose_values(value_batch)
             if h == 1:
                 close_sums(b - 1)
             if h == 2:
-                transpose_values(b + 1)
-                finish(b - 1)
+                transpose_gate(b - 1)

@@ -47,6 +47,9 @@ def tile_trendattentionlayer_pa_t_kernel(
         gate_banks = stack.enter_context(tc.psum_pool(name="gate_banks", bufs=1))
         stack.enter_context(tc.manual_schedule())
 
+        identity = const.tile([P, P], F32, name="identity")
+        make_identity(nc, identity[:])
+
         def load_rows(rows, name, copies):
             raw = loaded.tile([P, ROWS * WIDTH], BF16, name=name, bufs=copies)
             nc.sync.dma_start(out=raw[:].rearrange("p (r e) -> p r e", r=ROWS), in_=rows)
@@ -54,7 +57,8 @@ def tile_trendattentionlayer_pa_t_kernel(
 
         query_raw, key_raw, value_raw = {}, {}, {}
         weight_raw = loaded.tile([P, PACK * WIDTH], BF16, name="weight_raw")
-        bias = const.tile([P, WIDTH], BF16, name="bias")
+        bias_rows = const.tile([P, P], BF16, name="bias_rows")
+        nc.gpsimd.memset(bias_rows[:], 0.0)
         for b in range(BATCH):
             queries = q_proj[b].rearrange("(p j) e -> p j e", j=QUERY_TILES)
             for h in range(GROUPS_PER_BATCH):
@@ -65,6 +69,10 @@ def tile_trendattentionlayer_pa_t_kernel(
                 query_raw[b * GROUPS_PER_BATCH + h] = load_rows(
                     queries[:, h * ROWS : (h + 1) * ROWS, :], "query_raw", N_GROUPS
                 )
+                if b == 0 and h == 0:
+                    nc.sync.dma_start(
+                        out=bias_rows[0 : WIDTH // P, :], in_=bv.rearrange("(i n) -> i n", n=P)
+                    )
             value_raw[b] = load_rows(
                 values[b].rearrange("(p r) e -> p r e", r=ROWS), "value_raw", BATCH
             )
@@ -73,10 +81,10 @@ def tile_trendattentionlayer_pa_t_kernel(
                     out=weight_raw[:].rearrange("w (u e n) -> w u e n", u=HALVES, e=2),
                     in_=Wv.rearrange("(u w e) n -> w u e n", u=HALVES, e=2),
                 )
-                nc.sync.dma_start(out=bias[:], in_=bv.partition_broadcast(P))
 
-        identity = const.tile([P, P], F32, name="identity")
-        make_identity(nc, identity[:])
+
+        identity_bf16 = const.tile([P, P], BF16, name="identity_bf16")
+        make_identity(nc, identity_bf16[:])
         ones_f32 = const.tile([P, P], F32, name="ones_f32")
         nc.gpsimd.memset(ones_f32[:], 1.0)
         uses = const.tile([P, QUERY_TILES], F32, name="uses")
@@ -145,7 +153,7 @@ def tile_trendattentionlayer_pa_t_kernel(
 
         def transpose_values(b):
             if 0 <= b < BATCH:
-                value_grouped[b] = transpose_rows(value_raw[b], "key_value_grouped", False)
+                value_grouped[b] = transpose_rows(value_raw[b], "key_value_grouped", True)
 
         def quantise_values(b):
             if 0 <= b < BATCH:
@@ -263,7 +271,28 @@ def tile_trendattentionlayer_pa_t_kernel(
                 out=gate_rows[b][:], lhsT=ones_f32[:], rhs=partial_sums[b][:], start=False, stop=True
             )
             gate_copies[b] = results.tile([P, KEYS], F32, name="gate_copy")
-            nc.scalar.copy(out=gate_copies[b][:], in_=gate_rows[b][:])
+            nc.scalar.copy(
+                out=gate_copies[b][:].rearrange("x (i p) -> x i p", i=KEY_TILES),
+                in_=gate_rows[b][:].rearrange("x (p i) -> x i p", i=KEY_TILES),
+            )
+
+        bias_columns = const.tile([P, WIDTH // P], F32, name="bias_columns")
+        bias = const.tile([P, WIDTH], F32, name="bias")
+
+        def stand_bias_up():
+            bank = transposed.tile([P, P], BF16, name="bank")
+            nc.tensor.transpose(bank[:], bias_rows[:], identity_bf16[:])
+            nc.vector.tensor_copy(out=bias_columns[:], in_=bank[:, 0 : WIDTH // P])
+
+        def spread_bias():
+            bank = transposed.tile([P, WIDTH], F32, name="bank")
+            for i in range(WIDTH // P):
+                nc.tensor.transpose(
+                    bank[:, i * P : (i + 1) * P],
+                    bias_columns[:, i : i + 1].to_broadcast([P, P]),
+                    identity[:],
+                )
+            nc.scalar.copy(out=bias[:], in_=bank[:])
 
         def quantise_weights():
             weight_grouped = operands.tile([P, WIDTH * PACK], BF16, name="weight_grouped", bufs=1, align_bytes=64)
@@ -316,7 +345,7 @@ def tile_trendattentionlayer_pa_t_kernel(
                 nc.scalar.activation(
                     out=v[:, i, :], in_=v[:, i, :], func=FUNC.Copy, scale=gates[b][:, i : i + 1]
                 )
-            nc.sync.dma_start(out=out[b].rearrange("(i p) e -> p i e", p=P), in_=v[:])
+            nc.sync.dma_start(out=out[b].rearrange("(p i) e -> p i e", i=KEY_TILES), in_=v[:])
 
         for t in range(-3, N_GROUPS + 4):
             b, h = divmod(t, GROUPS_PER_BATCH)
@@ -348,3 +377,7 @@ def tile_trendattentionlayer_pa_t_kernel(
                 close_sums(b - 1)
             if h == 2:
                 transpose_gate(b - 1)
+            if t == -1:
+                stand_bias_up()
+            if t == 0:
+                spread_bias()

@@ -19,13 +19,16 @@ WIDTH = 512
 STRIDES = (1, 2, 3)
 
 PACK = 4
-HALVES = 2
+PAIR = 2
+HALVES = WIDTH // PAIR // P
 ROWS = 4
+ROWS_PER_BANK = 2
 QUERY_TILES = QUERIES // P
 KEY_TILES = KEYS // P
 GROUPS_PER_BATCH = QUERY_TILES // ROWS
 N_GROUPS = BATCH * GROUPS_PER_BATCH
 VECTOR_TILES = 2
+ROUNDS_PER_PROJECTION = 4
 
 FLOPS = 2 * BATCH * (QUERIES * KEYS * WIDTH + KEYS * WIDTH * WIDTH)
 
@@ -47,51 +50,40 @@ def tile_trendattentionlayer_pa_t_kernel(
         gate_banks = stack.enter_context(tc.psum_pool(name="gate_banks", bufs=1))
         stack.enter_context(tc.manual_schedule())
 
-        identity = const.tile([P, P], F32, name="identity")
-        make_identity(nc, identity[:])
-
-        def load_rows(rows, name, copies):
+        def load_rows(dram_rows, name, copies):
             raw = loaded.tile([P, ROWS * WIDTH], BF16, name=name, bufs=copies)
-            nc.sync.dma_start(out=raw[:].rearrange("p (r e) -> p r e", r=ROWS), in_=rows)
+            nc.sync.dma_start(out=raw[:].rearrange("p (r e) -> p r e", r=ROWS), in_=dram_rows)
             return raw
 
         query_raw, key_raw, value_raw = {}, {}, {}
         weight_raw = loaded.tile([P, PACK * WIDTH], BF16, name="weight_raw")
-        bias_rows = const.tile([P, P], BF16, name="bias_rows")
-        nc.gpsimd.memset(bias_rows[:], 0.0)
+        bias = const.tile([P, WIDTH], BF16, name="bias")
         for b in range(BATCH):
             queries = q_proj[b].rearrange("(p j) e -> p j e", j=QUERY_TILES)
+            key_raw[b] = load_rows(k_proj[b].rearrange("(p r) e -> p r e", r=ROWS), "key_raw", BATCH)
             for h in range(GROUPS_PER_BATCH):
-                if h == 0:
-                    key_raw[b] = load_rows(
-                        k_proj[b].rearrange("(p r) e -> p r e", r=ROWS), "key_raw", BATCH
-                    )
                 query_raw[b * GROUPS_PER_BATCH + h] = load_rows(
                     queries[:, h * ROWS : (h + 1) * ROWS, :], "query_raw", N_GROUPS
                 )
-                if b == 0 and h == 0:
-                    nc.sync.dma_start(
-                        out=bias_rows[0 : WIDTH // P, :], in_=bv.rearrange("(i n) -> i n", n=P)
-                    )
             value_raw[b] = load_rows(
                 values[b].rearrange("(p r) e -> p r e", r=ROWS), "value_raw", BATCH
             )
             if b == 0:
                 nc.sync.dma_start(
-                    out=weight_raw[:].rearrange("w (u e n) -> w u e n", u=HALVES, e=2),
-                    in_=Wv.rearrange("(u w e) n -> w u e n", u=HALVES, e=2),
+                    out=weight_raw[:].rearrange("w (u c n) -> w u c n", u=HALVES, c=PAIR),
+                    in_=Wv.rearrange("(u w c) n -> w u c n", u=HALVES, c=PAIR),
                 )
+                nc.sync.dma_start(out=bias[:], in_=bv.partition_broadcast(P))
 
-
-        identity_bf16 = const.tile([P, P], BF16, name="identity_bf16")
-        make_identity(nc, identity_bf16[:])
-        ones_f32 = const.tile([P, P], F32, name="ones_f32")
-        nc.gpsimd.memset(ones_f32[:], 1.0)
+        identity = const.tile([P, P], F32, name="identity")
+        make_identity(nc, identity[:])
+        ones = const.tile([P, P], F32, name="ones")
+        nc.gpsimd.memset(ones[:], 1.0)
         uses = const.tile([P, QUERY_TILES], F32, name="uses")
-        nc.vector.memset(uses[:], 1.0)
-        nc.vector.memset(uses[:, 0:QUERY_TILES:2], 2.0)
-        nc.vector.memset(uses[:, 3:QUERY_TILES:6], 2.0)
-        nc.vector.memset(uses[:, 0:QUERY_TILES:6], 3.0)
+        nc.vector.memset(uses[:], 0.0)
+        for stride in STRIDES:
+            multiples = uses[:, 0:QUERY_TILES:stride]
+            nc.vector.tensor_scalar_add(out=multiples, in0=multiples, scalar1=1.0)
         warm = const.tile([P, 1], F32, name="warm")
         nc.vector.memset(warm[:], 0.0)
         warmed = const.tile([P, 1], F32, name="warmed")
@@ -101,34 +93,39 @@ def tile_trendattentionlayer_pa_t_kernel(
             grouped = operands.tile([P, ROWS * P * PACK], BF16, name=name, align_bytes=64)
             raw_words = raw[:].bitcast(F32)
             grouped_words = grouped[:].bitcast(F32)
-            for first in range(0, ROWS, 2):
-                bank = transposed.tile([P, 2 * HALVES * P], F32, name="bank")
-                for slot in range(2 * HALVES):
-                    source = (first * HALVES + slot) * P
+            for first_row in range(0, ROWS, ROWS_PER_BANK):
+                bank = transposed.tile([P, ROWS_PER_BANK * HALVES * P], F32, name="bank")
+                for slot in range(ROWS_PER_BANK * HALVES):
+                    source = (first_row * HALVES + slot) * P
                     nc.tensor.transpose(
                         bank[:, slot * P : (slot + 1) * P],
                         raw_words[:, source : source + P],
                         identity[:],
                     )
+                bank_rows = slice(first_row, first_row + ROWS_PER_BANK)
                 if columns_by_row:
                     nc.scalar.copy(
                         out=grouped_words.rearrange("w (r p u) -> w r p u", r=ROWS, u=HALVES)[
-                            :, first : first + 2, :, :
+                            :, bank_rows, :, :
                         ],
-                        in_=bank[:].rearrange("w (r u p) -> w r p u", r=2, u=HALVES),
+                        in_=bank[:].rearrange("w (r u p) -> w r p u", r=ROWS_PER_BANK, u=HALVES),
                     )
                 else:
                     nc.scalar.copy(
                         out=grouped_words.rearrange("w (p r u) -> w p r u", r=ROWS, u=HALVES)[
-                            :, :, first : first + 2, :
+                            :, :, bank_rows, :
                         ],
-                        in_=bank[:].rearrange("w (r u p) -> w p r u", r=2, u=HALVES),
+                        in_=bank[:].rearrange("w (r u p) -> w p r u", r=ROWS_PER_BANK, u=HALVES),
                     )
             return grouped
 
         def quantise(grouped, name, copies):
-            codes = operands.tile([P, ROWS * P], U32, name=name + "_codes", bufs=copies, align_bytes=64)
-            scales = operands.tile([P, ROWS * P], U8, name=name + "_scales", bufs=copies, align_bytes=64)
+            codes = operands.tile(
+                [P, ROWS * P], U32, name=name + "_codes", bufs=copies, align_bytes=64
+            )
+            scales = operands.tile(
+                [P, ROWS * P], U8, name=name + "_scales", bufs=copies, align_bytes=64
+            )
             nc.vector.quantize_mx(out=codes[:].bitcast(FP8X4), scales=scales[:], in_=grouped[:])
             return codes, scales
 
@@ -153,14 +150,24 @@ def tile_trendattentionlayer_pa_t_kernel(
 
         def transpose_values(b):
             if 0 <= b < BATCH:
-                value_grouped[b] = transpose_rows(value_raw[b], "key_value_grouped", True)
+                value_grouped[b] = transpose_rows(value_raw[b], "key_value_grouped", False)
 
         def quantise_values(b):
             if 0 <= b < BATCH:
                 value_mx[b] = quantise(value_grouped[b], "value", 2)
 
+        def quantise_weights():
+            weight_grouped = operands.tile(
+                [P, WIDTH * PACK], BF16, name="weight_grouped", bufs=1, align_bytes=64
+            )
+            nc.vector.tensor_copy(
+                out=weight_grouped[:].rearrange("w (n t) -> w n t", t=PACK),
+                in_=weight_raw[:].rearrange("w (t n) -> w n t", t=PACK),
+            )
+            weight_mx[0] = quantise(weight_grouped, "weight", 1)
+
         scores, tops, shifts, exponentials, shares = {}, {}, {}, {}, {}
-        partial_sums, gate_rows, gate_copies, projected = {}, {}, {}, {}
+        partial_sums, gate_rows, gate_copies, gates, projected = {}, {}, {}, {}, {}
 
         def multiply_scores(g, r):
             if not 0 <= g < N_GROUPS:
@@ -168,6 +175,7 @@ def tile_trendattentionlayer_pa_t_kernel(
             if r == 0:
                 scores[g] = results.tile([P, ROWS, KEYS], F32, name="attn", bufs=6)
                 tops[g] = stats.tile([P, ROWS], F32, name="top")
+                shifts[g] = stats.tile([P, ROWS], F32, name="shift")
             codes, scales = query_mx[g]
             key_codes, key_scales = key_mx[g // GROUPS_PER_BATCH]
             cols = slice(r * P, (r + 1) * P)
@@ -190,32 +198,40 @@ def tile_trendattentionlayer_pa_t_kernel(
                 op1=ALU.max,
                 accum_out=tops[g][:, r : r + 1],
             )
+            nc.gpsimd.tensor_scalar(
+                out=shifts[g][:, r : r + 1],
+                in0=tops[g][:, r : r + 1],
+                scalar1=-1.0,
+                scalar2=0.0,
+                op0=ALU.mult,
+                op1=ALU.add,
+            )
 
         def store_scores(g):
             if not 0 <= g < N_GROUPS:
                 return
             b, h = divmod(g, GROUPS_PER_BATCH)
-            shifts[g] = stats.tile([P, ROWS], F32, name="shift")
-            nc.vector.tensor_scalar_mul(out=shifts[g][:], in0=tops[g][:], scalar1=-1.0)
             for stride in STRIDES:
-                first = (-h * ROWS) % stride
-                count = len(range(first, ROWS, stride))
-                start_row = (h * ROWS + first) // stride
-                rows = attn_out[stride][b, 0].rearrange("(p r) s -> p r s", r=QUERY_TILES // stride)
+                first_tile = (-h * ROWS) % stride
+                count = len(range(first_tile, ROWS, stride))
+                first_out = (h * ROWS + first_tile) // stride
+                out_rows = attn_out[stride][b, 0].rearrange(
+                    "(p r) s -> p r s", r=QUERY_TILES // stride
+                )
                 nc.sync.dma_start(
-                    out=rows[:, start_row : start_row + count, :],
-                    in_=scores[g][:, first:ROWS:stride, :],
+                    out=out_rows[:, first_out : first_out + count, :],
+                    in_=scores[g][:, first_tile:ROWS:stride, :],
                 )
 
         def exponentiate(g):
             if not 0 <= g < N_GROUPS:
                 return
             h = g % GROUPS_PER_BATCH
-            e = results.tile([P, ROWS, KEYS], F32, name="e", bufs=3)
+            expo = results.tile([P, ROWS, KEYS], F32, name="expo", bufs=3)
             z = stats.tile([P, ROWS], F32, name="z")
             for r in range(ROWS):
                 nc.scalar.activation(
-                    out=e[:, r, :],
+                    out=expo[:, r, :],
                     in_=scores[g][:, r, :],
                     func=FUNC.Exp,
                     bias=shifts[g][:, r : r + 1],
@@ -225,8 +241,10 @@ def tile_trendattentionlayer_pa_t_kernel(
             inverse = stats.tile([P, ROWS], F32, name="inverse")
             nc.vector.reciprocal(out=inverse[:], in_=z[:])
             share = stats.tile([P, ROWS], F32, name="share")
-            nc.vector.tensor_mul(out=share[:], in0=inverse[:], in1=uses[:, h * ROWS : (h + 1) * ROWS])
-            exponentials[g], shares[g] = e, share
+            nc.vector.tensor_mul(
+                out=share[:], in0=inverse[:], in1=uses[:, h * ROWS : (h + 1) * ROWS]
+            )
+            exponentials[g], shares[g] = expo, share
 
         def add_on_vector(g, r):
             if not 0 <= g < N_GROUPS:
@@ -268,46 +286,29 @@ def tile_trendattentionlayer_pa_t_kernel(
             if not 0 <= b < BATCH:
                 return
             nc.tensor.matmul(
-                out=gate_rows[b][:], lhsT=ones_f32[:], rhs=partial_sums[b][:], start=False, stop=True
+                out=gate_rows[b][:], lhsT=ones[:], rhs=partial_sums[b][:], start=False, stop=True
             )
             gate_copies[b] = results.tile([P, KEYS], F32, name="gate_copy")
-            nc.scalar.copy(
-                out=gate_copies[b][:].rearrange("x (i p) -> x i p", i=KEY_TILES),
-                in_=gate_rows[b][:].rearrange("x (p i) -> x i p", i=KEY_TILES),
+            nc.scalar.copy(out=gate_copies[b][:], in_=gate_rows[b][:])
+
+        def transpose_gate(b):
+            if not 0 <= b < BATCH:
+                return
+            bank = transposed.tile([P, KEY_TILES * P], F32, name="bank")
+            for i in range(KEY_TILES):
+                cols = slice(i * P, (i + 1) * P)
+                nc.tensor.transpose(bank[:, cols], gate_copies[b][:, cols], identity[:])
+            gates[b] = stats.tile([P, KEY_TILES], F32, name="gate")
+            nc.vector.tensor_scalar_mul(
+                out=gates[b][:], in0=bank[:, 0 : KEY_TILES * P : P], scalar1=1.0 / len(STRIDES)
             )
-
-        bias_columns = const.tile([P, WIDTH // P], F32, name="bias_columns")
-        bias = const.tile([P, WIDTH], F32, name="bias")
-
-        def stand_bias_up():
-            bank = transposed.tile([P, P], BF16, name="bank")
-            nc.tensor.transpose(bank[:], bias_rows[:], identity_bf16[:])
-            nc.vector.tensor_copy(out=bias_columns[:], in_=bank[:, 0 : WIDTH // P])
-
-        def spread_bias():
-            bank = transposed.tile([P, WIDTH], F32, name="bank")
-            for i in range(WIDTH // P):
-                nc.tensor.transpose(
-                    bank[:, i * P : (i + 1) * P],
-                    bias_columns[:, i : i + 1].to_broadcast([P, P]),
-                    identity[:],
-                )
-            nc.scalar.copy(out=bias[:], in_=bank[:])
-
-        def quantise_weights():
-            weight_grouped = operands.tile([P, WIDTH * PACK], BF16, name="weight_grouped", bufs=1, align_bytes=64)
-            nc.vector.tensor_copy(
-                out=weight_grouped[:].rearrange("w (n t) -> w n t", t=PACK),
-                in_=weight_raw[:].rearrange("w (t n) -> w n t", t=PACK),
-            )
-            weight_mx[0] = quantise(weight_grouped, "weight", 1)
 
         def project_values(b):
             if not 0 <= b < BATCH:
                 return
             codes, scales = value_mx[b]
             weight_codes, weight_scales = weight_mx[0]
-            v = results.tile([P, KEY_TILES, WIDTH], F32, name="v", bufs=2)
+            v = results.tile([P, KEY_TILES, WIDTH], F32, name="v")
             for i in range(KEY_TILES):
                 cols = slice(i * P, (i + 1) * P)
                 acc = products.tile([P, WIDTH], F32, name="acc")
@@ -323,33 +324,26 @@ def tile_trendattentionlayer_pa_t_kernel(
                 nc.vector.tensor_tensor(out=v[:, i, :], in0=acc[:], in1=bias[:], op=ALU.add)
             projected[b] = v
 
-        gates = {}
-
-        def transpose_gate(b):
-            if not 0 <= b < BATCH:
-                return
-            bank = transposed.tile([P, KEY_TILES * P], F32, name="bank")
-            for i in range(KEY_TILES):
-                cols = slice(i * P, (i + 1) * P)
-                nc.tensor.transpose(bank[:, cols], gate_copies[b][:, cols], identity[:])
-            gates[b] = stats.tile([P, KEY_TILES], F32, name="gate")
-            nc.vector.tensor_scalar_mul(
-                out=gates[b][:], in0=bank[:, 0 : KEY_TILES * P : P], scalar1=1.0 / len(STRIDES)
-            )
-
         def apply_gate(b):
             if not 0 <= b < BATCH:
                 return
             v = projected[b]
-            for i in range(KEY_TILES):
+            out_rows = out[b].rearrange("(i p) e -> p i e", p=P)
+            half = KEY_TILES // 2
+            for i in range(half):
                 nc.scalar.activation(
                     out=v[:, i, :], in_=v[:, i, :], func=FUNC.Copy, scale=gates[b][:, i : i + 1]
                 )
-            nc.sync.dma_start(out=out[b].rearrange("(p i) e -> p i e", i=KEY_TILES), in_=v[:])
+            for i in range(half, KEY_TILES):
+                nc.vector.tensor_scalar_mul(
+                    out=v[:, i, :], in0=v[:, i, :], scalar1=gates[b][:, i : i + 1]
+                )
+            nc.sync.dma_start(out=out_rows[:, half:KEY_TILES, :], in_=v[:, half:KEY_TILES, :])
+            nc.sync.dma_start(out=out_rows[:, 0:half, :], in_=v[:, 0:half, :])
 
         for t in range(-3, N_GROUPS + 4):
             b, h = divmod(t, GROUPS_PER_BATCH)
-            value_batch, value_step = divmod(t + 1, 4)
+            value_batch, value_step = divmod(t + 1, ROUNDS_PER_PROJECTION)
             if h == 1:
                 quantise_keys(b + 1)
             quantise_queries(t + 1)
@@ -377,7 +371,3 @@ def tile_trendattentionlayer_pa_t_kernel(
                 close_sums(b - 1)
             if h == 2:
                 transpose_gate(b - 1)
-            if t == -1:
-                stand_bias_up()
-            if t == 0:
-                spread_bias()

@@ -12,6 +12,7 @@ ALU = mybir.AluOpType
 FUNC = mybir.ActivationFunctionType
 
 P = 128
+QUADRANT = 32
 BATCH = 4
 QUERIES = 1536
 KEYS = 512
@@ -55,9 +56,14 @@ def tile_trendattentionlayer_pa_t_kernel(
             nc.sync.dma_start(out=raw[:].rearrange("p (r e) -> p r e", r=ROWS), in_=dram_rows)
             return raw
 
+        bias_row = const.tile([P, WIDTH], BF16, name="bias_row", align_bytes=64)
+        nc.gpsimd.memset(bias_row[:], 0.0)
+        nc.scalar.dma_start(
+            out=bias_row[0:P:QUADRANT, :], in_=bv.partition_broadcast(P // QUADRANT)
+        )
+
         query_raw, key_raw, value_raw = {}, {}, {}
         weight_raw = loaded.tile([P, PACK * WIDTH], BF16, name="weight_raw")
-        bias = const.tile([P, WIDTH], BF16, name="bias")
         for b in range(BATCH):
             queries = q_proj[b].rearrange("(p j) e -> p j e", j=QUERY_TILES)
             key_raw[b] = load_rows(k_proj[b].rearrange("(p r) e -> p r e", r=ROWS), "key_raw", BATCH)
@@ -73,7 +79,6 @@ def tile_trendattentionlayer_pa_t_kernel(
                     out=weight_raw[:].rearrange("w (u c n) -> w u c n", u=HALVES, c=PAIR),
                     in_=Wv.rearrange("(u w c) n -> w u c n", u=HALVES, c=PAIR),
                 )
-                nc.sync.dma_start(out=bias[:], in_=bv.partition_broadcast(P))
 
         identity = const.tile([P, P], F32, name="identity")
         make_identity(nc, identity[:])
@@ -88,6 +93,18 @@ def tile_trendattentionlayer_pa_t_kernel(
         nc.vector.memset(warm[:], 0.0)
         warmed = const.tile([P, 1], F32, name="warmed")
         nc.scalar.activation(out=warmed[:], in_=warm[:], func=FUNC.Exp)
+
+        bias_turned = const.tile([P, WIDTH], BF16, name="bias_turned", align_bytes=64)
+        bias_spread = const.tile([P, WIDTH], BF16, name="bias_spread", align_bytes=64)
+        bias = const.tile([P, WIDTH], BF16, name="bias", align_bytes=64)
+        nc.vector.transpose(bias_turned[:], bias_row[:])
+        nc.vector.tensor_copy(
+            out=bias_spread[:].rearrange("p (b j) -> p b j", j=QUADRANT),
+            in_=bias_turned[:]
+            .rearrange("p (b j) -> p b j", j=QUADRANT)[:, :, 0:1]
+            .to_broadcast([P, WIDTH // QUADRANT, QUADRANT]),
+        )
+        nc.vector.transpose(bias[:], bias_spread[:])
 
         def transpose_rows(raw, name, columns_by_row):
             grouped = operands.tile([P, ROWS * P * PACK], BF16, name=name, align_bytes=64)

@@ -51,34 +51,44 @@ def tile_trendattentionlayer_pa_t_kernel(
         gate_banks = stack.enter_context(tc.psum_pool(name="gate_banks", bufs=1))
         stack.enter_context(tc.manual_schedule())
 
-        def load_rows(dram_rows, name, copies):
-            raw = loaded.tile([P, ROWS * WIDTH], BF16, name=name, bufs=copies)
-            nc.sync.dma_start(out=raw[:].rearrange("p (r e) -> p r e", r=ROWS), in_=dram_rows)
-            return raw
-
         bias_row = const.tile([P, WIDTH], BF16, name="bias_row", align_bytes=64)
-        nc.gpsimd.memset(bias_row[:], 0.0)
-        nc.scalar.dma_start(
+        nc.vector.memset(bias_row[:], 0.0)
+
+        query_raw = loaded.tile([P, BATCH, QUERY_TILES * WIDTH], BF16, name="query_raw")
+        key_raw = loaded.tile([P, BATCH, ROWS * WIDTH], BF16, name="key_raw")
+        value_raw = loaded.tile([P, BATCH, ROWS * WIDTH], BF16, name="value_raw")
+        weight_raw = loaded.tile([P, PACK * WIDTH], BF16, name="weight_raw")
+
+        def load_queries(b, first, last):
+            nc.sync.dma_start(
+                out=query_raw[:, b, first * WIDTH : last * WIDTH],
+                in_=q_proj[b].rearrange("(p j) e -> p (j e)", j=QUERY_TILES)[
+                    :, first * WIDTH : last * WIDTH
+                ],
+            )
+
+        def load_batches(raw, dram, first, last):
+            nc.sync.dma_start(
+                out=raw[:, first:last, :],
+                in_=dram[first:last].rearrange("b (p r) e -> p b (r e)", r=ROWS),
+            )
+
+        load_batches(key_raw, k_proj, 0, 1)
+        nc.sync.dma_start(
             out=bias_row[0:P:QUADRANT, :], in_=bv.partition_broadcast(P // QUADRANT)
         )
-
-        query_raw, key_raw, value_raw = {}, {}, {}
-        weight_raw = loaded.tile([P, PACK * WIDTH], BF16, name="weight_raw")
-        for b in range(BATCH):
-            queries = q_proj[b].rearrange("(p j) e -> p j e", j=QUERY_TILES)
-            key_raw[b] = load_rows(k_proj[b].rearrange("(p r) e -> p r e", r=ROWS), "key_raw", BATCH)
-            for h in range(GROUPS_PER_BATCH):
-                query_raw[b * GROUPS_PER_BATCH + h] = load_rows(
-                    queries[:, h * ROWS : (h + 1) * ROWS, :], "query_raw", N_GROUPS
-                )
-            value_raw[b] = load_rows(
-                values[b].rearrange("(p r) e -> p r e", r=ROWS), "value_raw", BATCH
-            )
-            if b == 0:
-                nc.sync.dma_start(
-                    out=weight_raw[:].rearrange("w (u c n) -> w u c n", u=HALVES, c=PAIR),
-                    in_=Wv.rearrange("(u w c) n -> w u c n", u=HALVES, c=PAIR),
-                )
+        load_queries(0, 0, ROWS)
+        load_queries(0, ROWS, QUERY_TILES)
+        load_batches(value_raw, values, 0, 1)
+        nc.sync.dma_start(
+            out=weight_raw[:].rearrange("w (u c n) -> w u c n", u=HALVES, c=PAIR),
+            in_=Wv.rearrange("(u w c) n -> w u c n", u=HALVES, c=PAIR),
+        )
+        load_batches(key_raw, k_proj, 1, BATCH)
+        load_queries(1, 0, QUERY_TILES)
+        load_batches(value_raw, values, 1, BATCH)
+        for b in range(2, BATCH):
+            load_queries(b, 0, QUERY_TILES)
 
         identity = const.tile([P, P], F32, name="identity")
         make_identity(nc, identity[:])
@@ -108,7 +118,7 @@ def tile_trendattentionlayer_pa_t_kernel(
 
         def transpose_rows(raw, name, columns_by_row):
             grouped = operands.tile([P, ROWS * P * PACK], BF16, name=name, align_bytes=64)
-            raw_words = raw[:].bitcast(F32)
+            raw_words = raw.bitcast(F32)
             grouped_words = grouped[:].bitcast(F32)
             for first_row in range(0, ROWS, ROWS_PER_BANK):
                 bank = transposed.tile([P, ROWS_PER_BANK * HALVES * P], F32, name="bank")
@@ -151,7 +161,12 @@ def tile_trendattentionlayer_pa_t_kernel(
 
         def transpose_queries(g):
             if 0 <= g < N_GROUPS:
-                query_grouped[g] = transpose_rows(query_raw[g], "query_grouped", True)
+                b, h = divmod(g, GROUPS_PER_BATCH)
+                query_grouped[g] = transpose_rows(
+                    query_raw[:, b, h * ROWS * WIDTH : (h + 1) * ROWS * WIDTH],
+                    "query_grouped",
+                    True,
+                )
 
         def quantise_queries(g):
             if 0 <= g < N_GROUPS:
@@ -159,7 +174,7 @@ def tile_trendattentionlayer_pa_t_kernel(
 
         def transpose_keys(b):
             if 0 <= b < BATCH:
-                key_grouped[b] = transpose_rows(key_raw[b], "key_value_grouped", False)
+                key_grouped[b] = transpose_rows(key_raw[:, b, :], "key_value_grouped", False)
 
         def quantise_keys(b):
             if 0 <= b < BATCH:
@@ -167,7 +182,9 @@ def tile_trendattentionlayer_pa_t_kernel(
 
         def transpose_values(b):
             if 0 <= b < BATCH:
-                value_grouped[b] = transpose_rows(value_raw[b], "key_value_grouped", False)
+                value_grouped[b] = transpose_rows(
+                    value_raw[:, b, :], "key_value_grouped", False
+                )
 
         def quantise_values(b):
             if 0 <= b < BATCH:
@@ -189,12 +206,15 @@ def tile_trendattentionlayer_pa_t_kernel(
         def multiply_scores(g, r):
             if not 0 <= g < N_GROUPS:
                 return
+            b, h = divmod(g, GROUPS_PER_BATCH)
+            j = h * ROWS + r
+            if j == 0:
+                scores[b] = results.tile([P, QUERY_TILES, KEYS], F32, name="attn")
             if r == 0:
-                scores[g] = results.tile([P, ROWS, KEYS], F32, name="attn", bufs=6)
                 tops[g] = stats.tile([P, ROWS], F32, name="top")
                 shifts[g] = stats.tile([P, ROWS], F32, name="shift")
             codes, scales = query_mx[g]
-            key_codes, key_scales = key_mx[g // GROUPS_PER_BATCH]
+            key_codes, key_scales = key_mx[b]
             cols = slice(r * P, (r + 1) * P)
             acc = products.tile([P, KEYS], F32, name="acc")
             nc.tensor.matmul_mx(
@@ -207,7 +227,7 @@ def tile_trendattentionlayer_pa_t_kernel(
                 stop=True,
             )
             nc.vector.tensor_scalar(
-                out=scores[g][:, r, :],
+                out=scores[b][:, j, :],
                 in0=acc[:],
                 scalar1=1.0,
                 scalar2=None,
@@ -229,27 +249,30 @@ def tile_trendattentionlayer_pa_t_kernel(
                 return
             b, h = divmod(g, GROUPS_PER_BATCH)
             for stride in STRIDES:
-                first_tile = (-h * ROWS) % stride
-                count = len(range(first_tile, ROWS, stride))
-                first_out = (h * ROWS + first_tile) // stride
+                if stride == 1:
+                    tiles = slice(h * ROWS, (h + 1) * ROWS)
+                elif h == GROUPS_PER_BATCH - 1:
+                    tiles = slice(0, QUERY_TILES)
+                else:
+                    continue
                 out_rows = attn_out[stride][b, 0].rearrange(
                     "(p r) s -> p r s", r=QUERY_TILES // stride
                 )
                 nc.sync.dma_start(
-                    out=out_rows[:, first_out : first_out + count, :],
-                    in_=scores[g][:, first_tile:ROWS:stride, :],
+                    out=out_rows[:, tiles.start // stride : tiles.stop // stride, :],
+                    in_=scores[b][:, tiles.start : tiles.stop : stride, :],
                 )
 
         def exponentiate(g):
             if not 0 <= g < N_GROUPS:
                 return
-            h = g % GROUPS_PER_BATCH
+            b, h = divmod(g, GROUPS_PER_BATCH)
             expo = results.tile([P, ROWS, KEYS], F32, name="expo", bufs=3)
             z = stats.tile([P, ROWS], F32, name="z")
             for r in range(ROWS):
                 nc.scalar.activation(
                     out=expo[:, r, :],
-                    in_=scores[g][:, r, :],
+                    in_=scores[b][:, h * ROWS + r, :],
                     func=FUNC.Exp,
                     bias=shifts[g][:, r : r + 1],
                     scale=1.0,

@@ -77,19 +77,20 @@ def tile_trendattentionlayer_pa_t_kernel(
         nc.sync.dma_start(
             out=bias_row[0:P:QUADRANT, :], in_=bv.partition_broadcast(P // QUADRANT)
         )
-        load_queries(0, 0, ROWS)
-        load_queries(0, ROWS, QUERY_TILES)
+        load_queries(0, 0, 4)
+        load_queries(0, 4, 8)
+        load_queries(0, 8, 12)
+        load_batches(key_raw, k_proj, 1, 2)
+        load_queries(1, 0, 12)
         load_batches(value_raw, values, 0, 1)
         nc.sync.dma_start(
             out=weight_raw[:].rearrange("w (u c n) -> w u c n", u=HALVES, c=PAIR),
             in_=Wv.rearrange("(u w c) n -> w u c n", u=HALVES, c=PAIR),
         )
-        load_batches(key_raw, k_proj, 1, BATCH)
-        load_queries(1, 0, QUERY_TILES)
-        load_batches(value_raw, values, 1, BATCH)
-        for b in range(2, BATCH):
-            load_queries(b, 0, QUERY_TILES)
-
+        load_batches(value_raw, values, 1, 4)
+        load_batches(key_raw, k_proj, 2, 4)
+        load_queries(2, 0, 12)
+        load_queries(3, 0, 12)
         identity = const.tile([P, P], F32, name="identity")
         make_identity(nc, identity[:])
         ones = const.tile([P, P], F32, name="ones")
@@ -200,7 +201,8 @@ def tile_trendattentionlayer_pa_t_kernel(
             )
             weight_mx[0] = quantise(weight_grouped, "weight", 1)
 
-        scores, tops, shifts, exponentials, shares = {}, {}, {}, {}, {}
+        scores, tops, shifts, exponentials = {}, {}, {}, {}
+        row_sums, inverses, shares = {}, {}, {}
         partial_sums, gate_rows, gate_copies, gates, projected = {}, {}, {}, {}, {}
 
         def multiply_scores(g, r):
@@ -278,13 +280,21 @@ def tile_trendattentionlayer_pa_t_kernel(
                     scale=1.0,
                     accum_out=z[:, r : r + 1],
                 )
-            inverse = stats.tile([P, ROWS], F32, name="inverse")
-            nc.vector.reciprocal(out=inverse[:], in_=z[:])
-            share = stats.tile([P, ROWS], F32, name="share")
+            exponentials[g], row_sums[g] = expo, z
+
+        def take_shares(g, first=0, last=ROWS):
+            if not 0 <= g < N_GROUPS:
+                return
+            h = g % GROUPS_PER_BATCH
+            if first == 0:
+                shares[g] = stats.tile([P, ROWS], F32, name="share")
+                inverses[g] = stats.tile([P, ROWS], F32, name="inverse")
+            nc.vector.reciprocal(out=inverses[g][:, first:last], in_=row_sums[g][:, first:last])
             nc.vector.tensor_mul(
-                out=share[:], in0=inverse[:], in1=uses[:, h * ROWS : (h + 1) * ROWS]
+                out=shares[g][:, first:last],
+                in0=inverses[g][:, first:last],
+                in1=uses[:, h * ROWS + first : h * ROWS + last],
             )
-            exponentials[g], shares[g] = expo, share
 
         def add_on_vector(g, r):
             if not 0 <= g < N_GROUPS:
@@ -307,18 +317,18 @@ def tile_trendattentionlayer_pa_t_kernel(
                     op1=ALU.add,
                 )
 
-        def add_on_tensor(g):
+        def add_on_tensor(g, tiles):
             if not 0 <= g < N_GROUPS:
                 return
             b, h = divmod(g, GROUPS_PER_BATCH)
             if h == 0:
                 gate_rows[b] = gate_banks.tile([P, KEYS], F32, name="gate_row")
-            for r in range(VECTOR_TILES, ROWS):
+            for r in tiles:
                 nc.tensor.matmul(
                     out=gate_rows[b][:],
                     lhsT=shares[g][:, r : r + 1].to_broadcast([P, P]),
                     rhs=exponentials[g][:, r, :],
-                    start=(h == 0 and r == VECTOR_TILES),
+                    start=(h == 0 and r == tiles[0]),
                     stop=False,
                 )
 
@@ -383,7 +393,6 @@ def tile_trendattentionlayer_pa_t_kernel(
 
         for t in range(-3, N_GROUPS + 4):
             b, h = divmod(t, GROUPS_PER_BATCH)
-            value_batch, value_step = divmod(t + 1, ROUNDS_PER_PROJECTION)
             if h == 1:
                 quantise_keys(b + 1)
             quantise_queries(t + 1)
@@ -393,20 +402,21 @@ def tile_trendattentionlayer_pa_t_kernel(
                     add_on_vector(t - 2, r)
             store_scores(t)
             exponentiate(t - 1)
+            take_shares(t - 1)
             if h == 0:
                 apply_gate(b - 2)
             transpose_queries(t + 2)
-            add_on_tensor(t - 2)
-            if value_step == 2:
-                project_values(value_batch)
-            if value_step == 1:
-                if value_batch == 0:
+            add_on_tensor(t - 2, (2, 3))
+            if h == 0:
+                project_values(b - 1)
+            if h == 2:
+                if b == 0:
                     quantise_weights()
-                quantise_values(value_batch)
+                quantise_values(b)
             if h == 0:
                 transpose_keys(b + 1)
-            if value_step == 0:
-                transpose_values(value_batch)
+            if h == 1:
+                transpose_values(b)
             if h == 1:
                 close_sums(b - 1)
             if h == 2:

@@ -265,13 +265,15 @@ def tile_trendattentionlayer_pa_t_kernel(
                     in_=scores[b][:, tiles.start : tiles.stop : stride, :],
                 )
 
-        def exponentiate(g):
+        def exponentiate(g, half=None):
             if not 0 <= g < N_GROUPS:
                 return
             b, h = divmod(g, GROUPS_PER_BATCH)
-            expo = results.tile([P, ROWS, KEYS], F32, name="expo", bufs=3)
-            z = stats.tile([P, ROWS], F32, name="z")
-            for r in range(ROWS):
+            if half != 1:
+                exponentials[g] = results.tile([P, ROWS, KEYS], F32, name="expo", bufs=3)
+                row_sums[g] = stats.tile([P, ROWS], F32, name="z")
+            expo, z = exponentials[g], row_sums[g]
+            for r in range(ROWS) if half is None else range(2 * half, 2 * half + 2):
                 nc.scalar.activation(
                     out=expo[:, r, :],
                     in_=scores[b][:, h * ROWS + r, :],
@@ -280,7 +282,13 @@ def tile_trendattentionlayer_pa_t_kernel(
                     scale=1.0,
                     accum_out=z[:, r : r + 1],
                 )
-            exponentials[g], row_sums[g] = expo, z
+
+        def invert_sums(g, first=0, last=ROWS):
+            if not 0 <= g < N_GROUPS:
+                return
+            if first == 0:
+                inverses[g] = stats.tile([P, ROWS], F32, name="inverse")
+            nc.vector.reciprocal(out=inverses[g][:, first:last], in_=row_sums[g][:, first:last])
 
         def take_shares(g, first=0, last=ROWS):
             if not 0 <= g < N_GROUPS:
@@ -288,15 +296,13 @@ def tile_trendattentionlayer_pa_t_kernel(
             h = g % GROUPS_PER_BATCH
             if first == 0:
                 shares[g] = stats.tile([P, ROWS], F32, name="share")
-                inverses[g] = stats.tile([P, ROWS], F32, name="inverse")
-            nc.vector.reciprocal(out=inverses[g][:, first:last], in_=row_sums[g][:, first:last])
             nc.vector.tensor_mul(
                 out=shares[g][:, first:last],
                 in0=inverses[g][:, first:last],
                 in1=uses[:, h * ROWS + first : h * ROWS + last],
             )
 
-        def add_on_vector(g, r):
+        def add_on_vector(g, r, engine=None):
             if not 0 <= g < N_GROUPS:
                 return
             b, h = divmod(g, GROUPS_PER_BATCH)
@@ -338,6 +344,10 @@ def tile_trendattentionlayer_pa_t_kernel(
             nc.tensor.matmul(
                 out=gate_rows[b][:], lhsT=ones[:], rhs=partial_sums[b][:], start=False, stop=True
             )
+
+        def copy_sums(b):
+            if not 0 <= b < BATCH:
+                return
             gate_copies[b] = results.tile([P, KEYS], F32, name="gate_copy")
             nc.scalar.copy(out=gate_copies[b][:], in_=gate_rows[b][:])
 
@@ -358,7 +368,7 @@ def tile_trendattentionlayer_pa_t_kernel(
                 return
             codes, scales = value_mx[b]
             weight_codes, weight_scales = weight_mx[0]
-            v = results.tile([P, KEY_TILES, WIDTH], F32, name="v")
+            v = projected[b] = results.tile([P, KEY_TILES, WIDTH], F32, name="v")
             for i in range(KEY_TILES):
                 cols = slice(i * P, (i + 1) * P)
                 acc = products.tile([P, WIDTH], F32, name="acc")
@@ -372,14 +382,12 @@ def tile_trendattentionlayer_pa_t_kernel(
                     stop=True,
                 )
                 nc.vector.tensor_tensor(out=v[:, i, :], in0=acc[:], in1=bias[:], op=ALU.add)
-            projected[b] = v
 
-        def apply_gate(b):
+        def apply_gate(b, half=KEY_TILES // 2):
             if not 0 <= b < BATCH:
                 return
             v = projected[b]
             out_rows = out[b].rearrange("(i p) e -> p i e", p=P)
-            half = KEY_TILES // 2
             for i in range(half):
                 nc.scalar.activation(
                     out=v[:, i, :], in_=v[:, i, :], func=FUNC.Copy, scale=gates[b][:, i : i + 1]
@@ -388,23 +396,54 @@ def tile_trendattentionlayer_pa_t_kernel(
                 nc.vector.tensor_scalar_mul(
                     out=v[:, i, :], in0=v[:, i, :], scalar1=gates[b][:, i : i + 1]
                 )
-            nc.sync.dma_start(out=out_rows[:, half:KEY_TILES, :], in_=v[:, half:KEY_TILES, :])
-            nc.sync.dma_start(out=out_rows[:, 0:half, :], in_=v[:, 0:half, :])
+            nc.sync.dma_start(out=out_rows[:, :, :], in_=v[:, :, :])
 
-        for t in range(-3, N_GROUPS + 4):
+        def finish_last(b):
+            v = projected[b]
+            out_rows = out[b].rearrange("(i p) e -> p i e", p=P)
+            gate = stats.tile([P, KEY_TILES], F32, name="gate")
+            picked = results.tile([P, KEY_TILES, P], F32, name="picked", bufs=1)
+            for i in range(KEY_TILES):
+                nc.vector.scalar_tensor_tensor(
+                    out=picked[:, i, :],
+                    in0=gate_rows[b][:, i * P : (i + 1) * P],
+                    scalar=1.0 / len(STRIDES),
+                    in1=identity[:],
+                    op0=ALU.mult,
+                    op1=ALU.mult,
+                    accum_out=gate[:, i : i + 1],
+                )
+            half = KEY_TILES // 2
+            for i in range(half):
+                nc.scalar.activation(
+                    out=v[:, i, :], in_=v[:, i, :], func=FUNC.Copy, scale=gate[:, i : i + 1]
+                )
+                nc.vector.tensor_scalar_mul(
+                    out=v[:, half + i, :], in0=v[:, half + i, :], scalar1=gate[:, half + i : half + i + 1]
+                )
+                for k in (i, half + i):
+                    nc.sync.dma_start(out=out_rows[:, k : k + 1, :], in_=v[:, k : k + 1, :])
+
+        last = N_GROUPS - 1
+        for t in range(-3, N_GROUPS):
             b, h = divmod(t, GROUPS_PER_BATCH)
             if h == 1:
                 quantise_keys(b + 1)
             quantise_queries(t + 1)
-            for r in range(ROWS):
+            for r in range(ROWS - 1):
                 multiply_scores(t, r)
                 if r < VECTOR_TILES:
                     add_on_vector(t - 2, r)
+            exponentiate(t - 1, 0)
+            if h == 2:
+                copy_sums(b - 1)
+            exponentiate(t - 1, 1)
+            invert_sums(t - 1)
+            multiply_scores(t, ROWS - 1)
             store_scores(t)
-            exponentiate(t - 1)
             take_shares(t - 1)
             if h == 0:
-                apply_gate(b - 2)
+                apply_gate(b - 2, 4)
             transpose_queries(t + 2)
             add_on_tensor(t - 2, (2, 3))
             if h == 0:
@@ -421,3 +460,16 @@ def tile_trendattentionlayer_pa_t_kernel(
                 close_sums(b - 1)
             if h == 2:
                 transpose_gate(b - 1)
+        exponentiate(last)
+        add_on_vector(last - 1, 0)
+        add_on_vector(last - 1, 1)
+        invert_sums(last)
+        apply_gate(BATCH - 2, 4)
+        take_shares(last)
+        add_on_tensor(last - 1, (2, 3))
+        add_on_vector(last, 0)
+        add_on_vector(last, 1)
+        add_on_tensor(last, (2, 3))
+        project_values(BATCH - 1)
+        close_sums(BATCH - 1)
+        finish_last(BATCH - 1)

@@ -246,23 +246,24 @@ def tile_trendattentionlayer_pa_t_kernel(
                 op1=ALU.add,
             )
 
-        def store_scores(g):
+        def store_scores(g, queue, strides):
             if not 0 <= g < N_GROUPS:
                 return
             b, h = divmod(g, GROUPS_PER_BATCH)
-            for stride in STRIDES:
-                if stride == 1:
+            for stride in strides:
+                if stride == 1 or b >= 2:
                     tiles = slice(h * ROWS, (h + 1) * ROWS)
                 elif h == GROUPS_PER_BATCH - 1:
                     tiles = slice(0, QUERY_TILES)
                 else:
                     continue
+                js = [j for j in range(tiles.start, tiles.stop) if j % stride == 0]
                 out_rows = attn_out[stride][b, 0].rearrange(
                     "(p r) s -> p r s", r=QUERY_TILES // stride
                 )
-                nc.sync.dma_start(
-                    out=out_rows[:, tiles.start // stride : tiles.stop // stride, :],
-                    in_=scores[b][:, tiles.start : tiles.stop : stride, :],
+                queue.dma_start(
+                    out=out_rows[:, js[0] // stride : js[-1] // stride + 1, :],
+                    in_=scores[b][:, js[0] : js[-1] + 1 : stride, :],
                 )
 
         def exponentiate(g, half=None):
@@ -435,12 +436,13 @@ def tile_trendattentionlayer_pa_t_kernel(
                 if r < VECTOR_TILES:
                     add_on_vector(t - 2, r)
             exponentiate(t - 1, 0)
+            store_scores(t - 1, nc.scalar, STRIDES[1:])
             if h == 2:
                 copy_sums(b - 1)
             exponentiate(t - 1, 1)
             invert_sums(t - 1)
             multiply_scores(t, ROWS - 1)
-            store_scores(t)
+            store_scores(t, nc.sync, STRIDES[:1])
             take_shares(t - 1)
             if h == 0:
                 apply_gate(b - 2, 4)
@@ -461,6 +463,7 @@ def tile_trendattentionlayer_pa_t_kernel(
             if h == 2:
                 transpose_gate(b - 1)
         exponentiate(last)
+        store_scores(last, nc.scalar, STRIDES[1:])
         add_on_vector(last - 1, 0)
         add_on_vector(last - 1, 1)
         invert_sums(last)

@@ -54,14 +54,16 @@ def tile_trendattentionlayer_pa_t_kernel(
         bias_row = const.tile([P, WIDTH], BF16, name="bias_row", align_bytes=64)
         nc.vector.memset(bias_row[:], 0.0)
 
-        query_raw = loaded.tile([P, BATCH, QUERY_TILES * WIDTH], BF16, name="query_raw")
+        query_raw = {}
         key_raw = loaded.tile([P, BATCH, ROWS * WIDTH], BF16, name="key_raw")
         value_raw = loaded.tile([P, BATCH, ROWS * WIDTH], BF16, name="value_raw")
         weight_raw = loaded.tile([P, PACK * WIDTH], BF16, name="weight_raw")
 
         def load_queries(b, first, last):
+            if first == 0:
+                query_raw[b] = loaded.tile([P, QUERY_TILES * WIDTH], BF16, name="query_raw", bufs=3)
             nc.sync.dma_start(
-                out=query_raw[:, b, first * WIDTH : last * WIDTH],
+                out=query_raw[b][:, first * WIDTH : last * WIDTH],
                 in_=q_proj[b].rearrange("(p j) e -> p (j e)", j=QUERY_TILES)[
                     :, first * WIDTH : last * WIDTH
                 ],
@@ -81,16 +83,15 @@ def tile_trendattentionlayer_pa_t_kernel(
         load_queries(0, 4, 8)
         load_queries(0, 8, 12)
         load_batches(key_raw, k_proj, 1, 2)
-        load_queries(1, 0, 12)
-        load_batches(value_raw, values, 0, 1)
         nc.sync.dma_start(
             out=weight_raw[:].rearrange("w (u c n) -> w u c n", u=HALVES, c=PAIR),
             in_=Wv.rearrange("(u w c) n -> w u c n", u=HALVES, c=PAIR),
         )
+        load_queries(1, 0, 12)
+        load_batches(value_raw, values, 0, 1)
         load_batches(value_raw, values, 1, 4)
         load_batches(key_raw, k_proj, 2, 4)
         load_queries(2, 0, 12)
-        load_queries(3, 0, 12)
         identity = const.tile([P, P], F32, name="identity")
         make_identity(nc, identity[:])
         ones = const.tile([P, P], F32, name="ones")
@@ -164,7 +165,7 @@ def tile_trendattentionlayer_pa_t_kernel(
             if 0 <= g < N_GROUPS:
                 b, h = divmod(g, GROUPS_PER_BATCH)
                 query_grouped[g] = transpose_rows(
-                    query_raw[:, b, h * ROWS * WIDTH : (h + 1) * ROWS * WIDTH],
+                    query_raw[b][:, h * ROWS * WIDTH : (h + 1) * ROWS * WIDTH],
                     "query_grouped",
                     True,
                 )
@@ -211,7 +212,7 @@ def tile_trendattentionlayer_pa_t_kernel(
             b, h = divmod(g, GROUPS_PER_BATCH)
             j = h * ROWS + r
             if j == 0:
-                scores[b] = results.tile([P, QUERY_TILES, KEYS], F32, name="attn")
+                scores[b] = results.tile([P, QUERY_TILES, KEYS], F32, name="attn", bufs=3)
             if r == 0:
                 tops[g] = stats.tile([P, ROWS], F32, name="top")
                 shifts[g] = stats.tile([P, ROWS], F32, name="shift")
@@ -297,10 +298,11 @@ def tile_trendattentionlayer_pa_t_kernel(
             h = g % GROUPS_PER_BATCH
             if first == 0:
                 shares[g] = stats.tile([P, ROWS], F32, name="share")
-            nc.vector.tensor_mul(
+            nc.gpsimd.tensor_tensor(
                 out=shares[g][:, first:last],
                 in0=inverses[g][:, first:last],
                 in1=uses[:, h * ROWS + first : h * ROWS + last],
+                op=ALU.mult,
             )
 
         def add_on_vector(g, r, engine=None):
@@ -403,10 +405,10 @@ def tile_trendattentionlayer_pa_t_kernel(
             v = projected[b]
             out_rows = out[b].rearrange("(i p) e -> p i e", p=P)
             gate = stats.tile([P, KEY_TILES], F32, name="gate")
-            picked = results.tile([P, KEY_TILES, P], F32, name="picked", bufs=1)
+            picked = results.tile([P, KEYS], F32, name="gate_copy")
             for i in range(KEY_TILES):
                 nc.vector.scalar_tensor_tensor(
-                    out=picked[:, i, :],
+                    out=picked[:, i * P : (i + 1) * P],
                     in0=gate_rows[b][:, i * P : (i + 1) * P],
                     scalar=1.0 / len(STRIDES),
                     in1=identity[:],
@@ -442,18 +444,20 @@ def tile_trendattentionlayer_pa_t_kernel(
             exponentiate(t - 1, 1)
             invert_sums(t - 1)
             multiply_scores(t, ROWS - 1)
-            store_scores(t, nc.sync, STRIDES[:1])
             take_shares(t - 1)
             if h == 0:
                 apply_gate(b - 2, 4)
             transpose_queries(t + 2)
+            if t == 0:
+                load_queries(BATCH - 1, 0, QUERY_TILES)
+            store_scores(t, nc.sync, STRIDES[:1])
             add_on_tensor(t - 2, (2, 3))
             if h == 0:
                 project_values(b - 1)
             if h == 2:
-                if b == 0:
-                    quantise_weights()
                 quantise_values(b)
+            if t == 0:
+                quantise_weights()
             if h == 0:
                 transpose_keys(b + 1)
             if h == 1:
@@ -472,7 +476,7 @@ def tile_trendattentionlayer_pa_t_kernel(
         add_on_tensor(last - 1, (2, 3))
         add_on_vector(last, 0)
         add_on_vector(last, 1)
-        add_on_tensor(last, (2, 3))
         project_values(BATCH - 1)
+        add_on_tensor(last, (2, 3))
         close_sums(BATCH - 1)
         finish_last(BATCH - 1)

@@ -205,6 +205,7 @@ def tile_trendattentionlayer_pa_t_kernel(
         scores, tops, shifts, exponentials = {}, {}, {}, {}
         row_sums, inverses, shares = {}, {}, {}
         partial_sums, gate_rows, gate_copies, gates, projected = {}, {}, {}, {}, {}
+        products_of = {}
 
         def multiply_scores(g, r):
             if not 0 <= g < N_GROUPS:
@@ -298,7 +299,8 @@ def tile_trendattentionlayer_pa_t_kernel(
             h = g % GROUPS_PER_BATCH
             if first == 0:
                 shares[g] = stats.tile([P, ROWS], F32, name="share")
-            nc.gpsimd.tensor_tensor(
+            engine = nc.gpsimd if g < N_GROUPS - 2 else nc.vector
+            engine.tensor_tensor(
                 out=shares[g][:, first:last],
                 in0=inverses[g][:, first:last],
                 in1=uses[:, h * ROWS + first : h * ROWS + last],
@@ -371,7 +373,7 @@ def tile_trendattentionlayer_pa_t_kernel(
                 return
             codes, scales = value_mx[b]
             weight_codes, weight_scales = weight_mx[0]
-            v = projected[b] = results.tile([P, KEY_TILES, WIDTH], F32, name="v")
+            products_of[b] = []
             for i in range(KEY_TILES):
                 cols = slice(i * P, (i + 1) * P)
                 acc = products.tile([P, WIDTH], F32, name="acc")
@@ -384,7 +386,16 @@ def tile_trendattentionlayer_pa_t_kernel(
                     start=True,
                     stop=True,
                 )
-                nc.vector.tensor_tensor(out=v[:, i, :], in0=acc[:], in1=bias[:], op=ALU.add)
+                products_of[b].append(acc)
+
+        def add_bias(b):
+            if not 0 <= b < BATCH:
+                return
+            v = projected[b] = results.tile([P, KEY_TILES, WIDTH], F32, name="v")
+            for i in range(KEY_TILES):
+                nc.vector.tensor_tensor(
+                    out=v[:, i, :], in0=products_of[b][i][:], in1=bias[:], op=ALU.add
+                )
 
         def apply_gate(b, half=KEY_TILES // 2):
             if not 0 <= b < BATCH:
@@ -454,6 +465,7 @@ def tile_trendattentionlayer_pa_t_kernel(
             add_on_tensor(t - 2, (2, 3))
             if h == 0:
                 project_values(b - 1)
+                add_bias(b - 1)
             if h == 2:
                 quantise_values(b)
             if t == 0:
@@ -468,6 +480,7 @@ def tile_trendattentionlayer_pa_t_kernel(
                 transpose_gate(b - 1)
         exponentiate(last)
         store_scores(last, nc.scalar, STRIDES[1:])
+        project_values(BATCH - 1)
         add_on_vector(last - 1, 0)
         add_on_vector(last - 1, 1)
         invert_sums(last)
@@ -476,7 +489,8 @@ def tile_trendattentionlayer_pa_t_kernel(
         add_on_tensor(last - 1, (2, 3))
         add_on_vector(last, 0)
         add_on_vector(last, 1)
-        project_values(BATCH - 1)
-        add_on_tensor(last, (2, 3))
+        add_on_vector(last, 2)
+        add_bias(BATCH - 1)
+        add_on_tensor(last, (3,))
         close_sums(BATCH - 1)
         finish_last(BATCH - 1)

@@ -449,7 +449,6 @@ def tile_trendattentionlayer_pa_t_kernel(
                 if r < VECTOR_TILES:
                     add_on_vector(t - 2, r)
             exponentiate(t - 1, 0)
-            store_scores(t - 1, nc.scalar, STRIDES[1:])
             if h == 2:
                 copy_sums(b - 1)
             exponentiate(t - 1, 1)
@@ -461,7 +460,7 @@ def tile_trendattentionlayer_pa_t_kernel(
             transpose_queries(t + 2)
             if t == 0:
                 load_queries(BATCH - 1, 0, QUERY_TILES)
-            store_scores(t, nc.sync, STRIDES[:1])
+            store_scores(t, nc.sync, STRIDES)
             add_on_tensor(t - 2, (2, 3))
             if h == 0:
                 project_values(b - 1)
@@ -479,7 +478,6 @@ def tile_trendattentionlayer_pa_t_kernel(
             if h == 2:
                 transpose_gate(b - 1)
         exponentiate(last)
-        store_scores(last, nc.scalar, STRIDES[1:])
         project_values(BATCH - 1)
         add_on_vector(last - 1, 0)
         add_on_vector(last - 1, 1)

from contextlib import ExitStack

import concourse.mybir as mybir
from concourse.masks import make_identity

F32 = mybir.dt.float32
BF16 = mybir.dt.bfloat16
U32 = mybir.dt.uint32
U8 = mybir.dt.uint8
FP8X4 = mybir.dt.float8_e4m3fn_x4
ALU = mybir.AluOpType
FUNC = mybir.ActivationFunctionType

P = 128
QUADRANT = 32
BATCH = 4
QUERIES = 1536
KEYS = 512
WIDTH = 512
STRIDES = (1, 2, 3)

PACK = 4
PAIR = 2
HALVES = WIDTH // PAIR // P
ROWS = 4
ROWS_PER_BANK = 2
QUERY_TILES = QUERIES // P
KEY_TILES = KEYS // P
GROUPS_PER_BATCH = QUERY_TILES // ROWS
N_GROUPS = BATCH * GROUPS_PER_BATCH
VECTOR_TILES = 2
ROUNDS_PER_PROJECTION = 4

FLOPS = 2 * BATCH * (QUERIES * KEYS * WIDTH + KEYS * WIDTH * WIDTH)


def tile_trendattentionlayer_pa_t_kernel(
    tc, q_proj, k_proj, values, Wv, bv, out, attn_1, attn_2, attn_3
):
    nc = tc.nc
    attn_out = {1: attn_1, 2: attn_2, 3: attn_3}

    with ExitStack() as stack:
        const = stack.enter_context(tc.tile_pool(name="const", bufs=1))
        loaded = stack.enter_context(tc.tile_pool(name="loaded", bufs=1))
        operands = stack.enter_context(tc.tile_pool(name="operands", bufs=2))
        results = stack.enter_context(tc.tile_pool(name="results", bufs=2))
        stats = stack.enter_context(tc.tile_pool(name="stats", bufs=3))
        transposed = stack.enter_context(tc.psum_pool(name="transposed", bufs=2))
        products = stack.enter_context(tc.psum_pool(name="products", bufs=5))
        gate_banks = stack.enter_context(tc.psum_pool(name="gate_banks", bufs=1))
        stack.enter_context(tc.manual_schedule())

        bias_row = const.tile([P, WIDTH], BF16, name="bias_row", align_bytes=64)
        nc.vector.memset(bias_row[:], 0.0)

        query_raw = {}
        key_raw = loaded.tile([P, BATCH, ROWS * WIDTH], BF16, name="key_raw")
        value_raw = loaded.tile([P, BATCH, ROWS * WIDTH], BF16, name="value_raw")
        weight_raw = loaded.tile([P, PACK * WIDTH], BF16, name="weight_raw")

        def load_queries(b, first, last):
            if first == 0:
                query_raw[b] = loaded.tile([P, QUERY_TILES * WIDTH], BF16, name="query_raw", bufs=3)
            nc.sync.dma_start(
                out=query_raw[b][:, first * WIDTH : last * WIDTH],
                in_=q_proj[b].rearrange("(p j) e -> p (j e)", j=QUERY_TILES)[
                    :, first * WIDTH : last * WIDTH
                ],
            )

        def load_batches(raw, dram, first, last):
            nc.sync.dma_start(
                out=raw[:, first:last, :],
                in_=dram[first:last].rearrange("b (p r) e -> p b (r e)", r=ROWS),
            )

        load_batches(key_raw, k_proj, 0, 1)
        nc.sync.dma_start(
            out=bias_row[0:P:QUADRANT, :], in_=bv.partition_broadcast(P // QUADRANT)
        )
        load_queries(0, 0, 4)
        load_queries(0, 4, 8)
        load_queries(0, 8, 12)
        load_batches(key_raw, k_proj, 1, 2)
        nc.sync.dma_start(
            out=weight_raw[:].rearrange("w (u c n) -> w u c n", u=HALVES, c=PAIR),
            in_=Wv.rearrange("(u w c) n -> w u c n", u=HALVES, c=PAIR),
        )
        load_queries(1, 0, 12)
        load_batches(value_raw, values, 0, 1)
        load_batches(value_raw, values, 1, 4)
        load_batches(key_raw, k_proj, 2, 4)
        load_queries(2, 0, 12)
        identity = const.tile([P, P], F32, name="identity")
        make_identity(nc, identity[:])
        ones = const.tile([P, P], F32, name="ones")
        nc.gpsimd.memset(ones[:], 1.0)
        uses = const.tile([P, QUERY_TILES], F32, name="uses")
        nc.vector.memset(uses[:], 0.0)
        for stride in STRIDES:
            multiples = uses[:, 0:QUERY_TILES:stride]
            nc.vector.tensor_scalar_add(out=multiples, in0=multiples, scalar1=1.0)
        warm = const.tile([P, 1], F32, name="warm")
        nc.vector.memset(warm[:], 0.0)
        warmed = const.tile([P, 1], F32, name="warmed")
        nc.scalar.activation(out=warmed[:], in_=warm[:], func=FUNC.Exp)

        bias_turned = const.tile([P, WIDTH], BF16, name="bias_turned", align_bytes=64)
        bias_spread = const.tile([P, WIDTH], BF16, name="bias_spread", align_bytes=64)
        bias = const.tile([P, WIDTH], BF16, name="bias", align_bytes=64)
        nc.vector.transpose(bias_turned[:], bias_row[:])
        nc.vector.tensor_copy(
            out=bias_spread[:].rearrange("p (b j) -> p b j", j=QUADRANT),
            in_=bias_turned[:]
            .rearrange("p (b j) -> p b j", j=QUADRANT)[:, :, 0:1]
            .to_broadcast([P, WIDTH // QUADRANT, QUADRANT]),
        )
        nc.vector.transpose(bias[:], bias_spread[:])

        def transpose_rows(raw, name, columns_by_row):
            grouped = operands.tile([P, ROWS * P * PACK], BF16, name=name, align_bytes=64)
            raw_words = raw.bitcast(F32)
            grouped_words = grouped[:].bitcast(F32)
            for first_row in range(0, ROWS, ROWS_PER_BANK):
                bank = transposed.tile([P, ROWS_PER_BANK * HALVES * P], F32, name="bank")
                for slot in range(ROWS_PER_BANK * HALVES):
                    source = (first_row * HALVES + slot) * P
                    nc.tensor.transpose(
                        bank[:, slot * P : (slot + 1) * P],
                        raw_words[:, source : source + P],
                        identity[:],
                    )
                bank_rows = slice(first_row, first_row + ROWS_PER_BANK)
                if columns_by_row:
                    nc.scalar.copy(
                        out=grouped_words.rearrange("w (r p u) -> w r p u", r=ROWS, u=HALVES)[
                            :, bank_rows, :, :
                        ],
                        in_=bank[:].rearrange("w (r u p) -> w r p u", r=ROWS_PER_BANK, u=HALVES),
                    )
                else:
                    nc.scalar.copy(
                        out=grouped_words.rearrange("w (p r u) -> w p r u", r=ROWS, u=HALVES)[
                            :, :, bank_rows, :
                        ],
                        in_=bank[:].rearrange("w (r u p) -> w p r u", r=ROWS_PER_BANK, u=HALVES),
                    )
            return grouped

        def quantise(grouped, name, copies):
            codes = operands.tile(
                [P, ROWS * P], U32, name=name + "_codes", bufs=copies, align_bytes=64
            )
            scales = operands.tile(
                [P, ROWS * P], U8, name=name + "_scales", bufs=copies, align_bytes=64
            )
            nc.vector.quantize_mx(out=codes[:].bitcast(FP8X4), scales=scales[:], in_=grouped[:])
            return codes, scales

        query_grouped, key_grouped, value_grouped = {}, {}, {}
        query_mx, key_mx, value_mx, weight_mx = {}, {}, {}, {}

        def transpose_queries(g):
            if 0 <= g < N_GROUPS:
                b, h = divmod(g, GROUPS_PER_BATCH)
                query_grouped[g] = transpose_rows(
                    query_raw[b][:, h * ROWS * WIDTH : (h + 1) * ROWS * WIDTH],
                    "query_grouped",
                    True,
                )

        def quantise_queries(g):
            if 0 <= g < N_GROUPS:
                query_mx[g] = quantise(query_grouped[g], "query", 3)

        def transpose_keys(b):
            if 0 <= b < BATCH:
                key_grouped[b] = transpose_rows(key_raw[:, b, :], "key_value_grouped", False)

        def quantise_keys(b):
            if 0 <= b < BATCH:
                key_mx[b] = quantise(key_grouped[b], "key", 2)

        def transpose_values(b):
            if 0 <= b < BATCH:
                value_grouped[b] = transpose_rows(
                    value_raw[:, b, :], "key_value_grouped", False
                )

        def quantise_values(b):
            if 0 <= b < BATCH:
                value_mx[b] = quantise(value_grouped[b], "value", 2)

        def quantise_weights():
            weight_grouped = operands.tile(
                [P, WIDTH * PACK], BF16, name="weight_grouped", bufs=1, align_bytes=64
            )
            nc.vector.tensor_copy(
                out=weight_grouped[:].rearrange("w (n t) -> w n t", t=PACK),
                in_=weight_raw[:].rearrange("w (t n) -> w n t", t=PACK),
            )
            weight_mx[0] = quantise(weight_grouped, "weight", 1)

        scores, tops, shifts, exponentials = {}, {}, {}, {}
        row_sums, inverses, shares = {}, {}, {}
        partial_sums, gate_rows, gate_copies, gates, projected = {}, {}, {}, {}, {}
        products_of = {}

        def multiply_scores(g, r):
            if not 0 <= g < N_GROUPS:
                return
            b, h = divmod(g, GROUPS_PER_BATCH)
            j = h * ROWS + r
            if j == 0:
                scores[b] = results.tile([P, QUERY_TILES, KEYS], F32, name="attn", bufs=3)
            if r == 0:
                tops[g] = stats.tile([P, ROWS], F32, name="top")
                shifts[g] = stats.tile([P, ROWS], F32, name="shift")
            codes, scales = query_mx[g]
            key_codes, key_scales = key_mx[b]
            cols = slice(r * P, (r + 1) * P)
            acc = products.tile([P, KEYS], F32, name="acc")
            nc.tensor.matmul_mx(
                out=acc[:],
                lhsT=codes[:, cols].bitcast(FP8X4),
                lhsT_scale=scales[:, cols],
                rhs=key_codes[:].bitcast(FP8X4),
                rhs_scale=key_scales[:],
                start=True,
                stop=True,
            )
            nc.vector.tensor_scalar(
                out=scores[b][:, j, :],
                in0=acc[:],
                scalar1=1.0,
                scalar2=None,
                op0=ALU.mult,
                op1=ALU.max,
                accum_out=tops[g][:, r : r + 1],
            )
            nc.gpsimd.tensor_scalar(
                out=shifts[g][:, r : r + 1],
                in0=tops[g][:, r : r + 1],
                scalar1=-1.0,
                scalar2=0.0,
                op0=ALU.mult,
                op1=ALU.add,
            )

        def store_scores(g, queue, strides):
            if not 0 <= g < N_GROUPS:
                return
            b, h = divmod(g, GROUPS_PER_BATCH)
            for stride in strides:
                if stride == 1 or b >= 2:
                    tiles = slice(h * ROWS, (h + 1) * ROWS)
                elif h == GROUPS_PER_BATCH - 1:
                    tiles = slice(0, QUERY_TILES)
                else:
                    continue
                js = [j for j in range(tiles.start, tiles.stop) if j % stride == 0]
                out_rows = attn_out[stride][b, 0].rearrange(
                    "(p r) s -> p r s", r=QUERY_TILES // stride
                )
                queue.dma_start(
                    out=out_rows[:, js[0] // stride : js[-1] // stride + 1, :],
                    in_=scores[b][:, js[0] : js[-1] + 1 : stride, :],
                )

        def exponentiate(g, half=None):
            if not 0 <= g < N_GROUPS:
                return
            b, h = divmod(g, GROUPS_PER_BATCH)
            if half != 1:
                exponentials[g] = results.tile([P, ROWS, KEYS], F32, name="expo", bufs=3)
                row_sums[g] = stats.tile([P, ROWS], F32, name="z")
            expo, z = exponentials[g], row_sums[g]
            for r in range(ROWS) if half is None else range(2 * half, 2 * half + 2):
                nc.scalar.activation(
                    out=expo[:, r, :],
                    in_=scores[b][:, h * ROWS + r, :],
                    func=FUNC.Exp,
                    bias=shifts[g][:, r : r + 1],
                    scale=1.0,
                    accum_out=z[:, r : r + 1],
                )

        def invert_sums(g, first=0, last=ROWS):
            if not 0 <= g < N_GROUPS:
                return
            if first == 0:
                inverses[g] = stats.tile([P, ROWS], F32, name="inverse")
            nc.vector.reciprocal(out=inverses[g][:, first:last], in_=row_sums[g][:, first:last])

        def take_shares(g, first=0, last=ROWS):
            if not 0 <= g < N_GROUPS:
                return
            h = g % GROUPS_PER_BATCH
            if first == 0:
                shares[g] = stats.tile([P, ROWS], F32, name="share")
            engine = nc.gpsimd if g < N_GROUPS - 2 else nc.vector
            engine.tensor_tensor(
                out=shares[g][:, first:last],
                in0=inverses[g][:, first:last],
                in1=uses[:, h * ROWS + first : h * ROWS + last],
                op=ALU.mult,
            )

        def add_on_vector(g, r, engine=None):
            if not 0 <= g < N_GROUPS:
                return
            b, h = divmod(g, GROUPS_PER_BATCH)
            if h == 0 and r == 0:
                partial_sums[b] = results.tile([P, KEYS], F32, name="partial_sum")
                nc.vector.tensor_scalar_mul(
                    out=partial_sums[b][:],
                    in0=exponentials[g][:, r, :],
                    scalar1=shares[g][:, r : r + 1],
                )
            else:
                nc.vector.scalar_tensor_tensor(
                    out=partial_sums[b][:],
                    in0=exponentials[g][:, r, :],
                    scalar=shares[g][:, r : r + 1],
                    in1=partial_sums[b][:],
                    op0=ALU.mult,
                    op1=ALU.add,
                )

        def add_on_tensor(g, tiles):
            if not 0 <= g < N_GROUPS:
                return
            b, h = divmod(g, GROUPS_PER_BATCH)
            if h == 0:
                gate_rows[b] = gate_banks.tile([P, KEYS], F32, name="gate_row")
            for r in tiles:
                nc.tensor.matmul(
                    out=gate_rows[b][:],
                    lhsT=shares[g][:, r : r + 1].to_broadcast([P, P]),
                    rhs=exponentials[g][:, r, :],
                    start=(h == 0 and r == tiles[0]),
                    stop=False,
                )

        def close_sums(b):
            if not 0 <= b < BATCH:
                return
            nc.tensor.matmul(
                out=gate_rows[b][:], lhsT=ones[:], rhs=partial_sums[b][:], start=False, stop=True
            )

        def copy_sums(b):
            if not 0 <= b < BATCH:
                return
            gate_copies[b] = results.tile([P, KEYS], F32, name="gate_copy")
            nc.scalar.copy(out=gate_copies[b][:], in_=gate_rows[b][:])

        def transpose_gate(b):
            if not 0 <= b < BATCH:
                return
            bank = transposed.tile([P, KEY_TILES * P], F32, name="bank")
            for i in range(KEY_TILES):
                cols = slice(i * P, (i + 1) * P)
                nc.tensor.transpose(bank[:, cols], gate_copies[b][:, cols], identity[:])
            gates[b] = stats.tile([P, KEY_TILES], F32, name="gate")
            nc.vector.tensor_scalar_mul(
                out=gates[b][:], in0=bank[:, 0 : KEY_TILES * P : P], scalar1=1.0 / len(STRIDES)
            )

        def project_values(b):
            if not 0 <= b < BATCH:
                return
            codes, scales = value_mx[b]
            weight_codes, weight_scales = weight_mx[0]
            products_of[b] = []
            for i in range(KEY_TILES):
                cols = slice(i * P, (i + 1) * P)
                acc = products.tile([P, WIDTH], F32, name="acc")
                nc.tensor.matmul_mx(
                    out=acc[:],
                    lhsT=codes[:, cols].bitcast(FP8X4),
                    lhsT_scale=scales[:, cols],
                    rhs=weight_codes[:].bitcast(FP8X4),
                    rhs_scale=weight_scales[:],
                    start=True,
                    stop=True,
                )
                products_of[b].append(acc)

        def add_bias(b):
            if not 0 <= b < BATCH:
                return
            v = projected[b] = results.tile([P, KEY_TILES, WIDTH], F32, name="v")
            for i in range(KEY_TILES):
                nc.vector.tensor_tensor(
                    out=v[:, i, :], in0=products_of[b][i][:], in1=bias[:], op=ALU.add
                )

        def apply_gate(b, half=KEY_TILES // 2):
            if not 0 <= b < BATCH:
                return
            v = projected[b]
            out_rows = out[b].rearrange("(i p) e -> p i e", p=P)
            for i in range(half):
                nc.scalar.activation(
                    out=v[:, i, :], in_=v[:, i, :], func=FUNC.Copy, scale=gates[b][:, i : i + 1]
                )
            for i in range(half, KEY_TILES):
                nc.vector.tensor_scalar_mul(
                    out=v[:, i, :], in0=v[:, i, :], scalar1=gates[b][:, i : i + 1]
                )
            nc.sync.dma_start(out=out_rows[:, :, :], in_=v[:, :, :])

        def finish_last(b):
            v = projected[b]
            out_rows = out[b].rearrange("(i p) e -> p i e", p=P)
            gate = stats.tile([P, KEY_TILES], F32, name="gate")
            picked = results.tile([P, KEYS], F32, name="gate_copy")
            for i in range(KEY_TILES):
                nc.vector.scalar_tensor_tensor(
                    out=picked[:, i * P : (i + 1) * P],
                    in0=gate_rows[b][:, i * P : (i + 1) * P],
                    scalar=1.0 / len(STRIDES),
                    in1=identity[:],
                    op0=ALU.mult,
                    op1=ALU.mult,
                    accum_out=gate[:, i : i + 1],
                )
            half = KEY_TILES // 2
            for i in range(half):
                nc.scalar.activation(
                    out=v[:, i, :], in_=v[:, i, :], func=FUNC.Copy, scale=gate[:, i : i + 1]
                )
                nc.vector.tensor_scalar_mul(
                    out=v[:, half + i, :], in0=v[:, half + i, :], scalar1=gate[:, half + i : half + i + 1]
                )
                for k in (i, half + i):
                    nc.sync.dma_start(out=out_rows[:, k : k + 1, :], in_=v[:, k : k + 1, :])

        last = N_GROUPS - 1
        for t in range(-3, N_GROUPS):
            b, h = divmod(t, GROUPS_PER_BATCH)
            if h == 1:
                quantise_keys(b + 1)
            quantise_queries(t + 1)
            for r in range(ROWS - 1):
                multiply_scores(t, r)
                if r < VECTOR_TILES:
                    add_on_vector(t - 2, r)
            exponentiate(t - 1, 0)
            if h == 2:
                copy_sums(b - 1)
            exponentiate(t - 1, 1)
            invert_sums(t - 1)
            multiply_scores(t, ROWS - 1)
            take_shares(t - 1)
            if h == 0:
                apply_gate(b - 2, 4)
            transpose_queries(t + 2)
            if t == 0:
                load_queries(BATCH - 1, 0, QUERY_TILES)
            store_scores(t, nc.sync, STRIDES)
            add_on_tensor(t - 2, (2, 3))
            if h == 0:
                project_values(b - 1)
                add_bias(b - 1)
            if h == 2:
                quantise_values(b)
            if t == 0:
                quantise_weights()
            if h == 0:
                transpose_keys(b + 1)
            if h == 1:
                transpose_values(b)
            if h == 1:
                close_sums(b - 1)
            if h == 2:
                transpose_gate(b - 1)
        exponentiate(last)
        project_values(BATCH - 1)
        add_on_vector(last - 1, 0)
        add_on_vector(last - 1, 1)
        invert_sums(last)
        apply_gate(BATCH - 2, 4)
        take_shares(last)
        add_on_tensor(last - 1, (2, 3))
        add_on_vector(last, 0)
        add_on_vector(last, 1)
        add_on_vector(last, 2)
        add_bias(BATCH - 1)
        add_on_tensor(last, (3,))
        close_sums(BATCH - 1)
        finish_last(BATCH - 1)
